import numpy as np
import ml_dtypes


def mxq(x, axis, fmt="e4m3"):
    dtype, down = {"e4m3": (ml_dtypes.float8_e4m3fn, 7), "e5m2": (ml_dtypes.float8_e5m2, 14)}[fmt]
    v = np.moveaxis(np.asarray(x, np.float32).astype(ml_dtypes.bfloat16).astype(np.float64), axis, -1)
    blocks = v.reshape(v.shape[:-1] + (-1, 32))
    amax = np.abs(blocks).max(-1, keepdims=True)
    byte = np.maximum(np.where(amax > 0, np.frexp(amax)[1] - 1 + 127, 0) - down, 1)
    scale = np.exp2(byte - 127.0)
    codes = (blocks / scale).astype(np.float32).astype(dtype).astype(np.float64)
    return np.moveaxis((codes * scale).reshape(v.shape), -1, axis)


WIDE = False


def mx_kscale(k):
    if not WIDE:
        return np.ones(k)
    levels = np.array([10, -10, 5, -5, 0])
    if k % 512:
        return np.exp2(np.random.permutation(np.resize(levels, k // 32))).repeat(32)
    a = np.empty((k // 512, 16))
    for p in range(k // 512):
        a[p, :8] = np.random.permutation(np.resize(levels, 8))
        for g in range(8):
            far = levels[np.abs(levels - a[p, g]) >= 10]
            a[p, g + 8] = far[np.random.randint(len(far))]
    return np.exp2(a.ravel()).repeat(32)


BF16 = ml_dtypes.bfloat16


def bf(x):
    return np.asarray(x, np.float32).astype(BF16)


def f64(x):
    return np.asarray(x).astype(np.float64)


B, S, HID, H, KV, D, WIN, QB, KSZ = 4, 2048, 1024, 2, 2, 64, 384, 128, 4
EPS = 1e-5
QD, KVD = H * D, KV * D
C = QD + 2 * KVD


def silu(v):
    return v / (1.0 + np.exp(-v))


def rmsnorm(v, w):
    return v * (1.0 / np.sqrt(np.mean(v * v, axis=-1, keepdims=True) + EPS)) * w


def rotate_half(v):
    h = v.shape[-1] // 2
    return np.concatenate([-v[..., h:], v[..., :h]], axis=-1)


def canon(v, w, b):
    vp = np.pad(v, ((0, 0), (KSZ - 1, 0), (0, 0)))
    y = sum(vp[:, k:k + S, :] * w[:, k] for k in range(KSZ))
    return silu(y + b) + v


def setup_inputs():
    s = mx_kscale(HID)
    sd = 1.0 / np.sqrt(HID)
    inv_freq = 1.0 / (1e6 ** (np.arange(0, D, 2) / D))
    emb = np.concatenate([np.arange(S)[:, None] * inv_freq[None, :]] * 2, axis=-1)
    return {"x": bf(np.random.standard_normal((B, S, HID)) * s),
            "cos": bf(np.cos(emb)), "sin": bf(np.sin(emb)),
            "q_w": bf(np.random.standard_normal((QD, HID)) * sd / s[None, :]),
            "k_w": bf(np.random.standard_normal((KVD, HID)) * sd / s[None, :]),
            "v_w": bf(np.random.standard_normal((KVD, HID)) * sd / s[None, :]),
            "q_norm_w": bf(1.0 + 0.1 * np.random.standard_normal(D)),
            "k_norm_w": bf(1.0 + 0.1 * np.random.standard_normal(D)),
            "canon_w": bf(np.random.standard_normal((C, KSZ)) * 0.5),
            "canon_bias": bf(np.random.standard_normal(C) * 0.3)}


def reference(x, cos, sin, q_w, k_w, v_w, q_norm_w, k_norm_w, canon_w, canon_bias):
    xm = mxq(f64(x), 2, "e4m3")
    q = (xm @ mxq(f64(q_w), 1, "e4m3").T).reshape(B, S, H, D)
    k = (xm @ mxq(f64(k_w), 1, "e4m3").T).reshape(B, S, KV, D)
    v = xm @ mxq(f64(v_w), 1, "e4m3").T
    q = rmsnorm(q, f64(q_norm_w))
    k = rmsnorm(k, f64(k_norm_w))
    u = np.concatenate([q.reshape(B, S, QD), k.reshape(B, S, KVD), v], axis=-1)
    z = canon(u, f64(canon_w), f64(canon_bias))
    q = z[..., :QD].reshape(B, S, H, D)
    k = z[..., QD:QD + KVD].reshape(B, S, KV, D)
    v = z[..., QD + KVD:].reshape(B, S, KV, D)
    c, sn = f64(cos)[:, None, :], f64(sin)[:, None, :]
    return q * c + rotate_half(q) * sn, k * c + rotate_half(k) * sn, v

@@ -1,0 +1,401 @@
+from contextlib import ExitStack
+
+import concourse.mybir as mybir
+from concourse.masks import make_identity
+
+F32 = mybir.dt.float32
+BF16 = mybir.dt.bfloat16
+U32 = mybir.dt.uint32
+U8 = mybir.dt.uint8
+FP8X4 = mybir.dt.float8_e4m3fn_x4
+ALU = mybir.AluOpType
+ACT = mybir.ActivationFunctionType
+
+P = 128
+BATCH, SEQ, HID = 4, 2048, 1024
+HEAD = 64
+HALF = HEAD // 2
+TAPS = 4
+EPS = 1e-5
+PASSES = HID // (4 * P)
+WORD_TILES = HID // (2 * P)
+CHUNK = 256
+SUBS = CHUNK // P
+CHUNKS_PER_SEQ = SEQ // CHUNK
+CHUNKS = BATCH * CHUNKS_PER_SEQ
+GROUPS = 3
+QK = 2 * P
+QK_HEADS = QK // HEAD
+HALO = 8
+
+FLOPS = 2 * BATCH * SEQ * HID * GROUPS * P
+
+
+def transpose_words(nc, bank, rows, ident):
+    words = rows.bitcast(F32)
+    for w in range(WORD_TILES):
+        g, u = divmod(w, 2)
+        nc.tensor.transpose(
+            bank[:, w, :], words[:, 2 * P * g + u : 2 * P * (g + 1) : 2], ident
+        )
+
+
+def words_by_pass(bank):
+    return bank.rearrange("p (g u) r -> p g r u", u=2)
+
+
+def tile_attention_pa_t_kernel(
+    tc, x, cos, sin, q_w, k_w, v_w, q_norm_w, k_norm_w, canon_w, canon_bias, out_0, out_1, out_2
+):
+    nc = tc.nc
+    x_rows = x.flatten_outer_dims()
+    out_rows = [o.rearrange("b s h d -> (b s) (h d)") for o in (out_0, out_1, out_2)]
+
+    with ExitStack() as ctx:
+        ctx.enter_context(tc.manual_schedule())
+        consts = ctx.enter_context(tc.tile_pool(name="consts", bufs=1))
+        x_pool = ctx.enter_context(tc.tile_pool(name="x_pool", bufs=4))
+        mx_pool = ctx.enter_context(tc.tile_pool(name="mx_pool", bufs=2))
+        norm_pool = ctx.enter_context(tc.tile_pool(name="norm_pool", bufs=3))
+        u_pool = ctx.enter_context(tc.tile_pool(name="u_pool", bufs=2))
+        conv_pool = ctx.enter_context(tc.tile_pool(name="conv_pool", bufs=2))
+        rope_pool = ctx.enter_context(tc.tile_pool(name="rope_pool", bufs=2))
+        out_pool = ctx.enter_context(tc.tile_pool(name="out_pool", bufs=3))
+        psum = ctx.enter_context(tc.psum_pool(name="psum", bufs=2))
+
+        ident = consts.tile([P, P], F32)
+        make_identity(nc, ident[:])
+
+        w_raw = consts.tile([P, GROUPS, HID], BF16)
+        for grp, w in enumerate((q_w, k_w, v_w)):
+            nc.sync.dma_start(out=w_raw[:, grp, :], in_=w)
+        conv_w_bf = consts.tile([P, GROUPS, TAPS], BF16)
+        nc.scalar.dma_start(out=conv_w_bf[:], in_=canon_w.rearrange("(g c) j -> c g j", g=GROUPS))
+        conv_b_bf = consts.tile([P, GROUPS, 1], BF16)
+        nc.scalar.dma_start(
+            out=conv_b_bf[:], in_=canon_bias.rearrange("(g c o) -> c g o", g=GROUPS, o=1)
+        )
+        norm_w_bf = []
+        for w in (q_norm_w, k_norm_w):
+            repeated = consts.tile([P, 1], BF16, name="norm_w_bf%d" % len(norm_w_bf))
+            for head in range(P // HEAD):
+                nc.scalar.dma_start(
+                    out=repeated[head * HEAD : (head + 1) * HEAD, :],
+                    in_=w.rearrange("(d o) -> d o", o=1),
+                )
+            norm_w_bf.append(repeated)
+        cos_sb = consts.tile([P, SEQ // P, HEAD], BF16)
+        nc.scalar.dma_start(out=cos_sb[:], in_=cos.rearrange("(j p) d -> p j d", p=P))
+        sin_sb = consts.tile([P, SEQ // P, HEAD], BF16)
+        nc.scalar.dma_start(out=sin_sb[:], in_=sin.rearrange("(j p) d -> p j d", p=P))
+
+        w_grouped = consts.tile([P, PASSES, GROUPS * P * 4], BF16, align_bytes=64)
+        w_grouped_words = w_grouped[:].bitcast(F32).rearrange("p g (m u) -> p g m u", u=2)
+        for grp in range(GROUPS):
+            w_bank = psum.tile([P, WORD_TILES, P], F32, tag="xt")
+            transpose_words(nc, w_bank, w_raw[:, grp, :], ident[:])
+            nc.scalar.copy(
+                out=w_grouped_words[:, :, grp * P : (grp + 1) * P, :], in_=words_by_pass(w_bank[:])
+            )
+        w_codes = consts.tile([P, PASSES, GROUPS * P], U32, align_bytes=64)
+        w_scales = consts.tile([P, PASSES, GROUPS * P], U8, align_bytes=64)
+        for g in range(PASSES):
+            for lo, hi in ((0, QK), (QK, QK + P)):
+                nc.vector.quantize_mx(
+                    out=w_codes[:, g, lo:hi].bitcast(FP8X4),
+                    scales=w_scales[:, g, lo:hi],
+                    in_=w_grouped[:, g, 4 * lo : 4 * hi],
+                )
+
+        conv_w = consts.tile([P, GROUPS, TAPS], F32)
+        nc.vector.tensor_copy(out=conv_w[:], in_=conv_w_bf[:])
+        conv_b = consts.tile([P, GROUPS, 1], F32)
+        nc.vector.tensor_copy(out=conv_b[:], in_=conv_b_bf[:])
+        norm_w = consts.tile([P, 2], F32)
+        for grp in range(2):
+            nc.vector.tensor_copy(out=norm_w[:, grp : grp + 1], in_=norm_w_bf[grp][:])
+        nc.vector.tensor_scalar_mul(
+            out=sin_sb[:, :, 0:HALF], in0=sin_sb[:, :, 0:HALF], scalar1=-1.0
+        )
+        minus_half = consts.tile([P, SUBS * QK_HEADS], F32)
+        nc.gpsimd.memset(minus_half[:], -0.5)
+
+        kept = {}
+
+        def missing(chunk):
+            return not 0 <= chunk < CHUNKS
+
+        def first_column(chunk):
+            return HALO + (chunk % CHUNKS_PER_SEQ) * CHUNK
+
+        def load_x(chunk):
+            if missing(chunk):
+                return
+            x_raw = x_pool.tile([P, SUBS, HID], BF16)
+            nc.sync.dma_start(
+                out=x_raw[:],
+                in_=x_rows[chunk * CHUNK : (chunk + 1) * CHUNK, :].rearrange("(n p) k -> p n k", p=P),
+            )
+            kept["x_raw", chunk] = x_raw
+
+        def transpose_x(chunk):
+            if missing(chunk):
+                return
+            x_raw = kept["x_raw", chunk]
+            x_grouped = mx_pool.tile([P, PASSES, CHUNK * 4], BF16, align_bytes=64)
+            x_grouped_words = x_grouped[:].bitcast(F32).rearrange("p g (t u) -> p g t u", u=2)
+            for n in range(SUBS):
+                x_bank = psum.tile([P, WORD_TILES, P], F32, tag="xt")
+                transpose_words(nc, x_bank, x_raw[:, n, :], ident[:])
+                nc.scalar.copy(
+                    out=x_grouped_words[:, :, n * P : (n + 1) * P, :], in_=words_by_pass(x_bank[:])
+                )
+            kept["x_grouped", chunk] = x_grouped
+
+        def quantise_x(chunk):
+            if missing(chunk):
+                return
+            x_codes = mx_pool.tile([P, PASSES, CHUNK], U32, align_bytes=64)
+            x_scales = mx_pool.tile([P, PASSES, CHUNK], U8, align_bytes=64)
+            nc.vector.quantize_mx(
+                out=x_codes[:].rearrange("p g t -> p (g t)").bitcast(FP8X4),
+                scales=x_scales[:].rearrange("p g t -> p (g t)"),
+                in_=kept["x_grouped", chunk][:].rearrange("p g c -> p (g c)"),
+            )
+            kept["x_codes", chunk] = x_codes
+            kept["x_scales", chunk] = x_scales
+
+        def products(chunk):
+            if missing(chunk):
+                return
+            x_codes = kept["x_codes", chunk]
+            x_scales = kept["x_scales", chunk]
+            qk_bank = psum.tile([P, SUBS, QK], F32, tag="qk", bufs=3)
+            for n in range(SUBS):
+                for g in range(PASSES):
+                    nc.tensor.matmul_mx(
+                        out=qk_bank[:, n, :],
+                        lhsT=x_codes[:, g, n * P : (n + 1) * P].bitcast(FP8X4),
+                        lhsT_scale=x_scales[:, g, n * P : (n + 1) * P],
+                        rhs=w_codes[:, g, 0:QK].bitcast(FP8X4),
+                        rhs_scale=w_scales[:, g, 0:QK],
+                        start=(g == 0),
+                        stop=(g == PASSES - 1),
+                    )
+            kept["qk_bank", chunk] = qk_bank
+            v_bank = psum.tile([P, CHUNK], F32, tag="cl", bufs=1)
+            for g in range(PASSES):
+                nc.tensor.matmul_mx(
+                    out=v_bank[:],
+                    lhsT=w_codes[:, g, QK : QK + P].bitcast(FP8X4),
+                    lhsT_scale=w_scales[:, g, QK : QK + P],
+                    rhs=x_codes[:, g, :].bitcast(FP8X4),
+                    rhs_scale=x_scales[:, g, :],
+                    start=(g == 0),
+                    stop=(g == PASSES - 1),
+                )
+            kept["v_bank", chunk] = v_bank
+
+        def by_head(qk):
+            return qk.rearrange("p n (h d) -> p (n h) d", d=HEAD)
+
+        def inverse_rms(chunk):
+            if missing(chunk):
+                return
+            qk_heads = by_head(kept["qk_bank", chunk][:])
+            squares = norm_pool.tile([P, SUBS * QK_HEADS, HEAD], F32)
+            mean_sq = norm_pool.tile([P, SUBS * QK_HEADS], F32)
+            for h in range(SUBS * QK_HEADS):
+                nc.scalar.activation(
+                    out=squares[:, h, :],
+                    in_=qk_heads[:, h, :],
+                    func=ACT.Square,
+                    scale=0.125,
+                    accum_out=mean_sq[:, h : h + 1],
+                )
+            shifted = norm_pool.tile([P, SUBS * QK_HEADS], F32)
+            nc.gpsimd.tensor_scalar(
+                out=shifted[:], in0=mean_sq[:], scalar1=1.0, scalar2=EPS, op0=ALU.mult, op1=ALU.add
+            )
+            rstd = norm_pool.tile([P, SUBS * QK_HEADS], F32)
+            nc.gpsimd.tensor_tensor(out=rstd[:], in0=shifted[:], in1=minus_half[:], op=ALU.pow)
+            kept["rstd", chunk] = rstd
+
+        def normalise(chunk):
+            if missing(chunk):
+                return
+            qk_normed = norm_pool.tile([P, SUBS, QK], F32)
+            nc.vector.tensor_tensor(
+                out=by_head(qk_normed[:]),
+                in0=by_head(kept["qk_bank", chunk][:]),
+                in1=kept["rstd", chunk][:].unsqueeze(2).to_broadcast([P, SUBS * QK_HEADS, HEAD]),
+                op=ALU.mult,
+            )
+            kept["qk_normed", chunk] = qk_normed
+
+        def u_of(chunk):
+            seq = chunk // CHUNKS_PER_SEQ
+            if ("u", seq) not in kept:
+                u = u_pool.tile([P, GROUPS, HALO + SEQ], F32)
+                nc.gpsimd.memset(u[:, :, 0:HALO], 0.0)
+                kept["u", seq] = u
+            return kept["u", seq]
+
+        def copy_v(chunk):
+            if missing(chunk):
+                return
+            first = first_column(chunk)
+            nc.scalar.copy(out=u_of(chunk)[:, 2, first : first + CHUNK], in_=kept["v_bank", chunk][:])
+
+        def qk_to_channels(chunk):
+            if missing(chunk):
+                return
+            first = first_column(chunk)
+            u_bank = psum.tile([P, 2, CHUNK], F32, tag="cl", bufs=1)
+            for grp in range(2):
+                for n in range(SUBS):
+                    nc.tensor.transpose(
+                        u_bank[:, grp, n * P : (n + 1) * P],
+                        kept["qk_normed", chunk][:, n, grp * P : (grp + 1) * P],
+                        ident[:],
+                    )
+            for grp in range(2):
+                nc.scalar.activation(
+                    out=u_of(chunk)[:, grp, first : first + CHUNK],
+                    in_=u_bank[:, grp, :],
+                    func=ACT.Copy,
+                    scale=norm_w[:, grp : grp + 1],
+                )
+
+        def last_tap(chunk):
+            if missing(chunk):
+                return
+            first = first_column(chunk)
+            conv = conv_pool.tile([P, GROUPS, CHUNK], F32)
+            for grp in range(GROUPS):
+                nc.scalar.activation(
+                    out=conv[:, grp, :],
+                    in_=u_of(chunk)[:, grp, first : first + CHUNK],
+                    func=ACT.Copy,
+                    scale=conv_w[:, grp, TAPS - 1 : TAPS],
+                )
+            kept["conv", chunk] = conv
+
+        def other_taps(chunk):
+            if missing(chunk):
+                return
+            conv = kept["conv", chunk]
+            for tap in range(TAPS - 1):
+                start = first_column(chunk) - (TAPS - 1 - tap)
+                for grp in range(GROUPS):
+                    nc.vector.scalar_tensor_tensor(
+                        out=conv[:, grp, :],
+                        in0=u_of(chunk)[:, grp, start : start + CHUNK],
+                        scalar=conv_w[:, grp, tap : tap + 1],
+                        in1=conv[:, grp, :],
+                        op0=ALU.mult,
+                        op1=ALU.add,
+                    )
+
+        def gate(chunk):
+            if missing(chunk):
+                return
+            gated = conv_pool.tile([P, GROUPS, CHUNK], F32)
+            for grp in range(GROUPS):
+                nc.scalar.activation(
+                    out=gated[:, grp, :],
+                    in_=kept["conv", chunk][:, grp, :],
+                    func=ACT.Silu,
+                    bias=conv_b[:, grp, :],
+                )
+            kept["gated", chunk] = gated
+
+        def z_to_tokens(region, chunk, grp, n):
+            first = first_column(chunk)
+            nc.tensor.matmul(
+                region,
+                lhsT=kept["gated", chunk][:, grp, n * P : (n + 1) * P],
+                rhs=ident[:],
+                is_transpose=True,
+                start=True,
+                stop=False,
+            )
+            nc.tensor.matmul(
+                region,
+                lhsT=u_of(chunk)[:, grp, first + n * P : first + (n + 1) * P],
+                rhs=ident[:],
+                is_transpose=True,
+                start=False,
+                stop=True,
+            )
+
+        def rows_of(out, chunk):
+            return out[chunk * CHUNK : (chunk + 1) * CHUNK, :].rearrange("(n p) c -> p n c", p=P)
+
+        def finish_v(chunk):
+            if missing(chunk):
+                return
+            zv_bank = psum.tile([P, SUBS, P], F32, tag="zt")
+            for n in range(SUBS):
+                z_to_tokens(zv_bank[:, n, :], chunk, 2, n)
+            v_out = out_pool.tile([P, SUBS, P], F32)
+            nc.scalar.copy(out=v_out[:], in_=zv_bank[:])
+            nc.sync.dma_start(out=rows_of(out_rows[2], chunk), in_=v_out[:])
+
+        def qk_to_tokens(chunk):
+            if missing(chunk):
+                return
+            z_bank = psum.tile([P, SUBS, QK], F32, tag="zt")
+            for n in range(SUBS):
+                for grp in range(2):
+                    z_to_tokens(z_bank[:, n, grp * P : (grp + 1) * P], chunk, grp, n)
+            kept["z_bank", chunk] = z_bank
+
+        def rotate(chunk):
+            if missing(chunk):
+                return
+            z = kept["z_bank", chunk][:].rearrange("p n (h d) -> p n h d", d=HEAD)
+            j = (chunk % CHUNKS_PER_SEQ) * SUBS
+            table_shape = [P, SUBS, QK_HEADS, HEAD]
+            cos_b = cos_sb[:, j : j + SUBS, :].unsqueeze(2).to_broadcast(table_shape)
+            sin_b = sin_sb[:, j : j + SUBS, :].unsqueeze(2).to_broadcast(table_shape)
+            straight = rope_pool.tile(table_shape, F32)
+            nc.vector.tensor_tensor(out=straight[:], in0=z, in1=cos_b, op=ALU.mult)
+            turned = rope_pool.tile(table_shape, F32)
+            nc.vector.tensor_tensor(
+                out=turned[:, :, :, 0:HALF],
+                in0=z[:, :, :, HALF:HEAD],
+                in1=sin_b[:, :, :, 0:HALF],
+                op=ALU.mult,
+            )
+            nc.vector.tensor_tensor(
+                out=turned[:, :, :, HALF:HEAD],
+                in0=z[:, :, :, 0:HALF],
+                in1=sin_b[:, :, :, HALF:HEAD],
+                op=ALU.mult,
+            )
+            qk_out = out_pool.tile([P, SUBS, QK], F32)
+            nc.vector.tensor_tensor(
+                out=qk_out[:].rearrange("p n (h d) -> p n h d", d=HEAD),
+                in0=straight[:],
+                in1=turned[:],
+                op=ALU.add,
+            )
+            nc.sync.dma_start(out=rows_of(out_rows[0], chunk), in_=qk_out[:, :, 0:P])
+            nc.sync.dma_start(out=rows_of(out_rows[1], chunk), in_=qk_out[:, :, P:QK])
+
+        for r in range(-5, CHUNKS + 4):
+            load_x(r + 5)
+            products(r)
+            inverse_rms(r)
+            copy_v(r)
+            quantise_x(r + 1)
+            transpose_x(r + 2)
+            other_taps(r - 3)
+            normalise(r - 1)
+            finish_v(r - 4)
+            qk_to_channels(r - 2)
+            last_tap(r - 2)
+            gate(r - 3)
+            qk_to_tokens(r - 4)
+            rotate(r - 4)

@@ -27,6 +27,7 @@ GROUPS = 3
 QK = 2 * P
 QK_HEADS = QK // HEAD
 HALO = 8
+SCALAR_V_TAPS = (2, 3)
 
 FLOPS = 2 * BATCH * SEQ * HID * GROUPS * P
 
@@ -62,6 +63,11 @@ def tile_attention_pa_t_kernel(
         rope_pool = ctx.enter_context(tc.tile_pool(name="rope_pool", bufs=2))
         out_pool = ctx.enter_context(tc.tile_pool(name="out_pool", bufs=3))
         psum = ctx.enter_context(tc.psum_pool(name="psum", bufs=2))
+
+        warm = consts.tile([P, 1], F32)
+        nc.vector.memset(warm[:], 0.0)
+        warmed = consts.tile([P, 1], F32)
+        nc.scalar.activation(out=warmed[:], in_=warm[:], func=ACT.Silu)
 
         ident = consts.tile([P, P], F32)
         make_identity(nc, ident[:])
@@ -267,12 +273,66 @@ def tile_attention_pa_t_kernel(
                     scale=norm_w[:, grp : grp + 1],
                 )
 
+        def v_products(chunk):
+            if missing(chunk):
+                return
+            weighted = conv_pool.tile([P, TAPS, CHUNK], F32)
+            for tap in range(TAPS):
+                start = first_column(chunk) - (TAPS - 1 - tap)
+                v_shifted = u_of(chunk)[:, 2, start : start + CHUNK]
+                if tap in SCALAR_V_TAPS:
+                    nc.scalar.activation(
+                        out=weighted[:, tap, :],
+                        in_=v_shifted,
+                        func=ACT.Identity,
+                        scale=conv_w[:, 2, tap : tap + 1],
+                        bias=conv_b[:, 2, :] if tap == TAPS - 1 else 0.0,
+                    )
+                else:
+                    nc.vector.tensor_scalar_mul(
+                        out=weighted[:, tap, :], in0=v_shifted, scalar1=conv_w[:, 2, tap : tap + 1]
+                    )
+            kept["weighted", chunk] = weighted
+
+        def v_to_tokens(chunk):
+            if missing(chunk):
+                return
+            first = first_column(chunk)
+            bank = psum.tile([P, 2, SUBS, P], F32, tag="zt")
+            for n in range(SUBS):
+                for tap in range(TAPS):
+                    nc.tensor.matmul(
+                        bank[:, 0, n, :],
+                        lhsT=kept["weighted", chunk][:, tap, n * P : (n + 1) * P],
+                        rhs=ident[:],
+                        is_transpose=True,
+                        start=(tap == 0),
+                        stop=(tap == TAPS - 1),
+                    )
+            for n in range(SUBS):
+                nc.tensor.transpose(
+                    bank[:, 1, n, :], u_of(chunk)[:, 2, first + n * P : first + (n + 1) * P], ident[:]
+                )
+            kept["v_tokens", chunk] = bank
+            gated_v = out_pool.tile([P, SUBS, P], F32)
+            nc.scalar.activation(out=gated_v[:], in_=bank[:, 0], func=ACT.Silu)
+            kept["gated_v", chunk] = gated_v
+
+        def finish_v(chunk):
+            if missing(chunk):
+                return
+            v_out = out_pool.tile([P, SUBS, P], F32)
+            nc.vector.tensor_tensor(
+                out=v_out[:], in0=kept["v_tokens", chunk][:, 1], in1=kept["gated_v", chunk][:], op=ALU.add
+            )
+            nc.sync.dma_start(out=rows_of(out_rows[2], chunk), in_=v_out[:])
+
         def last_tap(chunk):
             if missing(chunk):
                 return
             first = first_column(chunk)
-            conv = conv_pool.tile([P, GROUPS, CHUNK], F32)
-            for grp in range(GROUPS):
+            conv = conv_pool.tile([P, 2, CHUNK], F32)
+            for grp in range(2):
                 nc.scalar.activation(
                     out=conv[:, grp, :],
                     in_=u_of(chunk)[:, grp, first : first + CHUNK],
@@ -287,7 +347,7 @@ def tile_attention_pa_t_kernel(
             conv = kept["conv", chunk]
             for tap in range(TAPS - 1):
                 start = first_column(chunk) - (TAPS - 1 - tap)
-                for grp in range(GROUPS):
+                for grp in range(2):
                     nc.vector.scalar_tensor_tensor(
                         out=conv[:, grp, :],
                         in0=u_of(chunk)[:, grp, start : start + CHUNK],
@@ -300,8 +360,8 @@ def tile_attention_pa_t_kernel(
         def gate(chunk):
             if missing(chunk):
                 return
-            gated = conv_pool.tile([P, GROUPS, CHUNK], F32)
-            for grp in range(GROUPS):
+            gated = conv_pool.tile([P, 2, CHUNK], F32)
+            for grp in range(2):
                 nc.scalar.activation(
                     out=gated[:, grp, :],
                     in_=kept["conv", chunk][:, grp, :],
@@ -331,16 +391,6 @@ def tile_attention_pa_t_kernel(
 
         def rows_of(out, chunk):
             return out[chunk * CHUNK : (chunk + 1) * CHUNK, :].rearrange("(n p) c -> p n c", p=P)
-
-        def finish_v(chunk):
-            if missing(chunk):
-                return
-            zv_bank = psum.tile([P, SUBS, P], F32, tag="zt")
-            for n in range(SUBS):
-                z_to_tokens(zv_bank[:, n, :], chunk, 2, n)
-            v_out = out_pool.tile([P, SUBS, P], F32)
-            nc.scalar.copy(out=v_out[:], in_=zv_bank[:])
-            nc.sync.dma_start(out=rows_of(out_rows[2], chunk), in_=v_out[:])
 
         def qk_to_tokens(chunk):
             if missing(chunk):
@@ -392,8 +442,10 @@ def tile_attention_pa_t_kernel(
             quantise_x(r + 1)
             transpose_x(r + 2)
             other_taps(r - 3)
+            v_products(r - 1)
             normalise(r - 1)
-            finish_v(r - 4)
+            v_to_tokens(r - 2)
+            finish_v(r - 2)
             qk_to_channels(r - 2)
             last_tap(r - 2)
             gate(r - 3)

@@ -23,11 +23,16 @@ CHUNK = 256
 SUBS = CHUNK // P
 CHUNKS_PER_SEQ = SEQ // CHUNK
 CHUNKS = BATCH * CHUNKS_PER_SEQ
+SPAN = 2 * CHUNK
+SPAN_TILES = SPAN // P
+SPANS_PER_SEQ = SEQ // SPAN
+UNITS = 2 * BATCH * SPANS_PER_SEQ
+GROUP_HEADS = P // HEAD
 GROUPS = 3
 QK = 2 * P
 QK_HEADS = QK // HEAD
 HALO = 8
-SCALAR_V_TAPS = (2, 3)
+TENSOR_V_TAPS = (0, 1)
 
 FLOPS = 2 * BATCH * SEQ * HID * GROUPS * P
 
@@ -57,7 +62,7 @@ def tile_attention_pa_t_kernel(
         consts = ctx.enter_context(tc.tile_pool(name="consts", bufs=1))
         x_pool = ctx.enter_context(tc.tile_pool(name="x_pool", bufs=4))
         mx_pool = ctx.enter_context(tc.tile_pool(name="mx_pool", bufs=2))
-        norm_pool = ctx.enter_context(tc.tile_pool(name="norm_pool", bufs=3))
+        norm_pool = ctx.enter_context(tc.tile_pool(name="norm_pool", bufs=4))
         u_pool = ctx.enter_context(tc.tile_pool(name="u_pool", bufs=2))
         conv_pool = ctx.enter_context(tc.tile_pool(name="conv_pool", bufs=2))
         rope_pool = ctx.enter_context(tc.tile_pool(name="rope_pool", bufs=2))
@@ -85,22 +90,17 @@ def tile_attention_pa_t_kernel(
         for w in (q_norm_w, k_norm_w):
             repeated = consts.tile([P, 1], BF16, name="norm_w_bf%d" % len(norm_w_bf))
             for head in range(P // HEAD):
-                nc.scalar.dma_start(
+                nc.gpsimd.dma_start(
                     out=repeated[head * HEAD : (head + 1) * HEAD, :],
                     in_=w.rearrange("(d o) -> d o", o=1),
                 )
             norm_w_bf.append(repeated)
-        cos_sb = consts.tile([P, SEQ // P, HEAD], BF16)
-        nc.scalar.dma_start(out=cos_sb[:], in_=cos.rearrange("(j p) d -> p j d", p=P))
-        sin_sb = consts.tile([P, SEQ // P, HEAD], BF16)
-        nc.scalar.dma_start(out=sin_sb[:], in_=sin.rearrange("(j p) d -> p j d", p=P))
-
         w_grouped = consts.tile([P, PASSES, GROUPS * P * 4], BF16, align_bytes=64)
         w_grouped_words = w_grouped[:].bitcast(F32).rearrange("p g (m u) -> p g m u", u=2)
         for grp in range(GROUPS):
             w_bank = psum.tile([P, WORD_TILES, P], F32, tag="xt")
             transpose_words(nc, w_bank, w_raw[:, grp, :], ident[:])
-            nc.scalar.copy(
+            nc.vector.tensor_copy(
                 out=w_grouped_words[:, :, grp * P : (grp + 1) * P, :], in_=words_by_pass(w_bank[:])
             )
         w_codes = consts.tile([P, PASSES, GROUPS * P], U32, align_bytes=64)
@@ -112,19 +112,6 @@ def tile_attention_pa_t_kernel(
                     scales=w_scales[:, g, lo:hi],
                     in_=w_grouped[:, g, 4 * lo : 4 * hi],
                 )
-
-        conv_w = consts.tile([P, GROUPS, TAPS], F32)
-        nc.vector.tensor_copy(out=conv_w[:], in_=conv_w_bf[:])
-        conv_b = consts.tile([P, GROUPS, 1], F32)
-        nc.vector.tensor_copy(out=conv_b[:], in_=conv_b_bf[:])
-        norm_w = consts.tile([P, 2], F32)
-        for grp in range(2):
-            nc.vector.tensor_copy(out=norm_w[:, grp : grp + 1], in_=norm_w_bf[grp][:])
-        nc.vector.tensor_scalar_mul(
-            out=sin_sb[:, :, 0:HALF], in0=sin_sb[:, :, 0:HALF], scalar1=-1.0
-        )
-        minus_half = consts.tile([P, SUBS * QK_HEADS], F32)
-        nc.gpsimd.memset(minus_half[:], -0.5)
 
         kept = {}
 
@@ -253,46 +240,53 @@ def tile_attention_pa_t_kernel(
             first = first_column(chunk)
             nc.scalar.copy(out=u_of(chunk)[:, 2, first : first + CHUNK], in_=kept["v_bank", chunk][:])
 
-        def qk_to_channels(chunk):
-            if missing(chunk):
+        def no_unit(unit):
+            return not 0 <= unit < UNITS
+
+        def span_column(unit):
+            return HALO + (unit // 2 % SPANS_PER_SEQ) * SPAN
+
+        def u_of_unit(unit, start):
+            return u_of(unit // 2 * 2)[:, unit % 2, start : start + SPAN]
+
+        def qk_to_channels(unit):
+            if no_unit(unit):
                 return
-            first = first_column(chunk)
-            u_bank = psum.tile([P, 2, CHUNK], F32, tag="cl", bufs=1)
-            for grp in range(2):
-                for n in range(SUBS):
-                    nc.tensor.transpose(
-                        u_bank[:, grp, n * P : (n + 1) * P],
-                        kept["qk_normed", chunk][:, n, grp * P : (grp + 1) * P],
-                        ident[:],
-                    )
-            for grp in range(2):
-                nc.scalar.activation(
-                    out=u_of(chunk)[:, grp, first : first + CHUNK],
-                    in_=u_bank[:, grp, :],
-                    func=ACT.Copy,
-                    scale=norm_w[:, grp : grp + 1],
+            grp = unit % 2
+            u_bank = psum.tile([P, SPAN], F32, tag="cl", bufs=1)
+            for tile in range(SPAN_TILES):
+                chunk, n = unit // 2 * 2 + tile // SUBS, tile % SUBS
+                nc.tensor.transpose(
+                    u_bank[:, tile * P : (tile + 1) * P],
+                    kept["qk_normed", chunk][:, n, grp * P : (grp + 1) * P],
+                    ident[:],
                 )
+            nc.scalar.activation(
+                out=u_of_unit(unit, span_column(unit)),
+                in_=u_bank[:],
+                func=ACT.Copy,
+                scale=norm_w[:, grp : grp + 1],
+            )
 
         def v_products(chunk):
             if missing(chunk):
                 return
-            weighted = conv_pool.tile([P, TAPS, CHUNK], F32)
-            for tap in range(TAPS):
-                start = first_column(chunk) - (TAPS - 1 - tap)
-                v_shifted = u_of(chunk)[:, 2, start : start + CHUNK]
-                if tap in SCALAR_V_TAPS:
-                    nc.scalar.activation(
-                        out=weighted[:, tap, :],
-                        in_=v_shifted,
-                        func=ACT.Identity,
-                        scale=conv_w[:, 2, tap : tap + 1],
-                        bias=conv_b[:, 2, :] if tap == TAPS - 1 else 0.0,
-                    )
-                else:
-                    nc.vector.tensor_scalar_mul(
-                        out=weighted[:, tap, :], in0=v_shifted, scalar1=conv_w[:, 2, tap : tap + 1]
-                    )
-            kept["weighted", chunk] = weighted
+            first = first_column(chunk)
+            v_last = conv_pool.tile([P, CHUNK], F32)
+            nc.scalar.activation(
+                out=v_last[:],
+                in_=u_of(chunk)[:, 2, first : first + CHUNK],
+                func=ACT.Identity,
+                scale=conv_w[:, 2, 3:4],
+                bias=conv_b[:, 2, :],
+            )
+            v_third = conv_pool.tile([P, CHUNK], F32)
+            nc.vector.tensor_scalar_mul(
+                out=v_third[:],
+                in0=u_of(chunk)[:, 2, first - 1 : first - 1 + CHUNK],
+                scalar1=conv_w[:, 2, 2:3],
+            )
+            kept["weighted", chunk] = (v_third, v_last)
 
         def v_to_tokens(chunk):
             if missing(chunk):
@@ -300,14 +294,23 @@ def tile_attention_pa_t_kernel(
             first = first_column(chunk)
             bank = psum.tile([P, 2, SUBS, P], F32, tag="zt")
             for n in range(SUBS):
-                for tap in range(TAPS):
+                for tap in TENSOR_V_TAPS:
+                    start = first + n * P - (TAPS - 1 - tap)
                     nc.tensor.matmul(
                         bank[:, 0, n, :],
-                        lhsT=kept["weighted", chunk][:, tap, n * P : (n + 1) * P],
+                        lhsT=u_of(chunk)[:, 2, start : start + P],
+                        rhs=v_diag[:, tap, :],
+                        start=(tap == 0),
+                        stop=False,
+                    )
+                for weighted in kept["weighted", chunk]:
+                    nc.tensor.matmul(
+                        bank[:, 0, n, :],
+                        lhsT=weighted[:, n * P : (n + 1) * P],
                         rhs=ident[:],
                         is_transpose=True,
-                        start=(tap == 0),
-                        stop=(tap == TAPS - 1),
+                        start=False,
+                        stop=(weighted is kept["weighted", chunk][-1]),
                     )
             for n in range(SUBS):
                 nc.tensor.transpose(
@@ -325,129 +328,153 @@ def tile_attention_pa_t_kernel(
             nc.vector.tensor_tensor(
                 out=v_out[:], in0=kept["v_tokens", chunk][:, 1], in1=kept["gated_v", chunk][:], op=ALU.add
             )
-            nc.sync.dma_start(out=rows_of(out_rows[2], chunk), in_=v_out[:])
+            nc.sync.dma_start(out=rows_of(out_rows[2], chunk * CHUNK, SUBS), in_=v_out[:])
 
-        def last_tap(chunk):
-            if missing(chunk):
+        def last_tap(unit):
+            if no_unit(unit):
                 return
-            first = first_column(chunk)
-            conv = conv_pool.tile([P, 2, CHUNK], F32)
-            for grp in range(2):
-                nc.scalar.activation(
-                    out=conv[:, grp, :],
-                    in_=u_of(chunk)[:, grp, first : first + CHUNK],
-                    func=ACT.Copy,
-                    scale=conv_w[:, grp, TAPS - 1 : TAPS],
-                )
-            kept["conv", chunk] = conv
-
-        def other_taps(chunk):
-            if missing(chunk):
-                return
-            conv = kept["conv", chunk]
-            for tap in range(TAPS - 1):
-                start = first_column(chunk) - (TAPS - 1 - tap)
-                for grp in range(2):
-                    nc.vector.scalar_tensor_tensor(
-                        out=conv[:, grp, :],
-                        in0=u_of(chunk)[:, grp, start : start + CHUNK],
-                        scalar=conv_w[:, grp, tap : tap + 1],
-                        in1=conv[:, grp, :],
-                        op0=ALU.mult,
-                        op1=ALU.add,
-                    )
-
-        def gate(chunk):
-            if missing(chunk):
-                return
-            gated = conv_pool.tile([P, 2, CHUNK], F32)
-            for grp in range(2):
-                nc.scalar.activation(
-                    out=gated[:, grp, :],
-                    in_=kept["conv", chunk][:, grp, :],
-                    func=ACT.Silu,
-                    bias=conv_b[:, grp, :],
-                )
-            kept["gated", chunk] = gated
-
-        def z_to_tokens(region, chunk, grp, n):
-            first = first_column(chunk)
-            nc.tensor.matmul(
-                region,
-                lhsT=kept["gated", chunk][:, grp, n * P : (n + 1) * P],
-                rhs=ident[:],
-                is_transpose=True,
-                start=True,
-                stop=False,
+            conv = conv_pool.tile([P, SPAN], F32)
+            nc.scalar.activation(
+                out=conv[:],
+                in_=u_of_unit(unit, span_column(unit)),
+                func=ACT.Copy,
+                scale=conv_w[:, unit % 2, TAPS - 1 : TAPS],
             )
-            nc.tensor.matmul(
-                region,
-                lhsT=u_of(chunk)[:, grp, first + n * P : first + (n + 1) * P],
-                rhs=ident[:],
-                is_transpose=True,
-                start=False,
-                stop=True,
+            kept["conv", unit] = conv
+
+        def other_tap(unit, tap):
+            if no_unit(unit):
+                return
+            conv = kept["conv", unit]
+            nc.vector.scalar_tensor_tensor(
+                out=conv[:],
+                in0=u_of_unit(unit, span_column(unit) - (TAPS - 1 - tap)),
+                scalar=conv_w[:, unit % 2, tap : tap + 1],
+                in1=conv[:],
+                op0=ALU.mult,
+                op1=ALU.add,
             )
 
-        def rows_of(out, chunk):
-            return out[chunk * CHUNK : (chunk + 1) * CHUNK, :].rearrange("(n p) c -> p n c", p=P)
-
-        def qk_to_tokens(chunk):
-            if missing(chunk):
+        def gate(unit):
+            if no_unit(unit):
                 return
-            z_bank = psum.tile([P, SUBS, QK], F32, tag="zt")
-            for n in range(SUBS):
-                for grp in range(2):
-                    z_to_tokens(z_bank[:, n, grp * P : (grp + 1) * P], chunk, grp, n)
-            kept["z_bank", chunk] = z_bank
+            gated = conv_pool.tile([P, SPAN], F32)
+            nc.scalar.activation(
+                out=gated[:], in_=kept["conv", unit][:], func=ACT.Silu, bias=conv_b[:, unit % 2, :]
+            )
+            kept["gated", unit] = gated
 
-        def rotate(chunk):
-            if missing(chunk):
+        def rows_of(out, first, tiles):
+            return out[first : first + tiles * P, :].rearrange("(n p) c -> p n c", p=P)
+
+        def qk_to_tokens(unit):
+            if no_unit(unit):
                 return
-            z = kept["z_bank", chunk][:].rearrange("p n (h d) -> p n h d", d=HEAD)
-            j = (chunk % CHUNKS_PER_SEQ) * SUBS
-            table_shape = [P, SUBS, QK_HEADS, HEAD]
-            cos_b = cos_sb[:, j : j + SUBS, :].unsqueeze(2).to_broadcast(table_shape)
-            sin_b = sin_sb[:, j : j + SUBS, :].unsqueeze(2).to_broadcast(table_shape)
+            z_bank = psum.tile([P, SPAN_TILES, P], F32, tag="zt")
+            u = u_of_unit(unit, span_column(unit))
+            for tile in range(SPAN_TILES):
+                tokens = slice(tile * P, (tile + 1) * P)
+                nc.tensor.matmul(
+                    z_bank[:, tile, :],
+                    lhsT=kept["gated", unit][:, tokens],
+                    rhs=ident[:],
+                    is_transpose=True,
+                    start=True,
+                    stop=False,
+                )
+                nc.tensor.matmul(
+                    z_bank[:, tile, :],
+                    lhsT=u[:, tokens],
+                    rhs=ident[:],
+                    is_transpose=True,
+                    start=False,
+                    stop=True,
+                )
+            kept["z_bank", unit] = z_bank
+
+        def rotate(unit):
+            if no_unit(unit):
+                return
+            z = kept["z_bank", unit][:].rearrange("p n (h d) -> p n h d", d=HEAD)
+            j = (unit // 2 % SPANS_PER_SEQ) * SPAN_TILES
+            table_shape = [P, SPAN_TILES, GROUP_HEADS, HEAD]
+            cos_b = cos_sb[:, j : j + SPAN_TILES, :].unsqueeze(2).to_broadcast(table_shape)
+            sin_b = sin_sb[:, j : j + SPAN_TILES, :].unsqueeze(2).to_broadcast(table_shape)
             straight = rope_pool.tile(table_shape, F32)
             nc.vector.tensor_tensor(out=straight[:], in0=z, in1=cos_b, op=ALU.mult)
             turned = rope_pool.tile(table_shape, F32)
+            by_half = "p n h (s d) -> p n h s d"
             nc.vector.tensor_tensor(
-                out=turned[:, :, :, 0:HALF],
-                in0=z[:, :, :, HALF:HEAD],
-                in1=sin_b[:, :, :, 0:HALF],
+                out=turned[:].rearrange(by_half, s=2),
+                in0=z.rearrange(by_half, s=2)[:, :, :, ::-1, :],
+                in1=sin_b.rearrange(by_half, s=2),
                 op=ALU.mult,
             )
-            nc.vector.tensor_tensor(
-                out=turned[:, :, :, HALF:HEAD],
-                in0=z[:, :, :, 0:HALF],
-                in1=sin_b[:, :, :, HALF:HEAD],
-                op=ALU.mult,
-            )
-            qk_out = out_pool.tile([P, SUBS, QK], F32)
+            kept["rope", unit] = (straight, turned)
+
+        def rotated(unit):
+            if no_unit(unit):
+                return
+            straight, turned = kept["rope", unit]
+            qk_out = out_pool.tile([P, SPAN_TILES, P], F32)
             nc.vector.tensor_tensor(
                 out=qk_out[:].rearrange("p n (h d) -> p n h d", d=HEAD),
                 in0=straight[:],
                 in1=turned[:],
                 op=ALU.add,
             )
-            nc.sync.dma_start(out=rows_of(out_rows[0], chunk), in_=qk_out[:, :, 0:P])
-            nc.sync.dma_start(out=rows_of(out_rows[1], chunk), in_=qk_out[:, :, P:QK])
+            nc.sync.dma_start(
+                out=rows_of(out_rows[unit % 2], unit // 2 * SPAN, SPAN_TILES), in_=qk_out[:]
+            )
 
-        for r in range(-5, CHUNKS + 4):
+        def one_round(r):
             load_x(r + 5)
             products(r)
             inverse_rms(r)
             copy_v(r)
+            other_tap(r - 4, 0)
             quantise_x(r + 1)
+            other_tap(r - 4, 1)
             transpose_x(r + 2)
-            other_taps(r - 3)
             v_products(r - 1)
+            other_tap(r - 4, 2)
             normalise(r - 1)
             v_to_tokens(r - 2)
+            qk_to_channels(r - 3)
+            last_tap(r - 3)
+            gate(r - 4)
+            qk_to_tokens(r - 5)
+            rotate(r - 5)
             finish_v(r - 2)
-            qk_to_channels(r - 2)
-            last_tap(r - 2)
-            gate(r - 3)
-            qk_to_tokens(r - 4)
-            rotate(r - 4)
+            rotated(r - 5)
+
+        for r in range(-5, 0):
+            one_round(r)
+
+        cos_sb = consts.tile([P, SEQ // P, HEAD], BF16)
+        nc.scalar.dma_start(out=cos_sb[:], in_=cos.rearrange("(j p) d -> p j d", p=P))
+        sin_sb = consts.tile([P, SEQ // P, HEAD], BF16)
+        nc.scalar.dma_start(out=sin_sb[:], in_=sin.rearrange("(j p) d -> p j d", p=P))
+
+        conv_w = consts.tile([P, GROUPS, TAPS], F32)
+        nc.vector.tensor_copy(out=conv_w[:], in_=conv_w_bf[:])
+        conv_b = consts.tile([P, GROUPS, 1], F32)
+        nc.vector.tensor_copy(out=conv_b[:], in_=conv_b_bf[:])
+        v_diag = consts.tile([P, len(TENSOR_V_TAPS), P], F32)
+        for tap in TENSOR_V_TAPS:
+            nc.vector.tensor_scalar_mul(
+                out=v_diag[:, tap, :], in0=ident[:], scalar1=conv_w[:, 2, tap : tap + 1]
+            )
+        norm_w = consts.tile([P, 2], F32)
+        for grp in range(2):
+            nc.vector.tensor_copy(out=norm_w[:, grp : grp + 1], in_=norm_w_bf[grp][:])
+        minus_half = consts.tile([P, SUBS * QK_HEADS], F32)
+        nc.gpsimd.memset(minus_half[:], -0.5)
+
+        for r in range(0, 3):
+            one_round(r)
+        nc.vector.tensor_scalar_mul(
+            out=sin_sb[:, :, 0:HALF], in0=sin_sb[:, :, 0:HALF], scalar1=-1.0
+        )
+        for r in range(3, UNITS + 5):
+            one_round(r)

@@ -192,7 +192,7 @@ def tile_attention_pa_t_kernel(
         def by_head(qk):
             return qk.rearrange("p n (h d) -> p (n h) d", d=HEAD)
 
-        def inverse_rms(chunk):
+        def mean_squares(chunk):
             if missing(chunk):
                 return
             qk_heads = by_head(kept["qk_bank", chunk][:])
@@ -206,9 +206,14 @@ def tile_attention_pa_t_kernel(
                     scale=0.125,
                     accum_out=mean_sq[:, h : h + 1],
                 )
+            kept["mean_sq", chunk] = mean_sq
+
+        def raise_to_power(chunk):
+            if missing(chunk):
+                return
             shifted = norm_pool.tile([P, SUBS * QK_HEADS], F32)
-            nc.gpsimd.tensor_scalar(
-                out=shifted[:], in0=mean_sq[:], scalar1=1.0, scalar2=EPS, op0=ALU.mult, op1=ALU.add
+            nc.scalar.activation(
+                out=shifted[:], in_=kept["mean_sq", chunk][:], func=ACT.Copy, bias=EPS
             )
             rstd = norm_pool.tile([P, SUBS * QK_HEADS], F32)
             nc.gpsimd.tensor_tensor(out=rstd[:], in0=shifted[:], in1=minus_half[:], op=ALU.pow)
@@ -430,8 +435,9 @@ def tile_attention_pa_t_kernel(
         def one_round(r):
             load_x(r + 5)
             products(r)
-            inverse_rms(r)
+            mean_squares(r)
             copy_v(r)
+            raise_to_power(r)
             other_tap(r - 4, 0)
             quantise_x(r + 1)
             other_tap(r - 4, 1)

@@ -266,6 +266,7 @@ def tile_attention_pa_t_kernel(
                     kept["qk_normed", chunk][:, n, grp * P : (grp + 1) * P],
                     ident[:],
                 )
+            kept["u_bank", unit] = u_bank
             nc.scalar.activation(
                 out=u_of_unit(unit, span_column(unit)),
                 in_=u_bank[:],
@@ -286,10 +287,10 @@ def tile_attention_pa_t_kernel(
                 bias=conv_b[:, 2, :],
             )
             v_third = conv_pool.tile([P, CHUNK], F32)
-            nc.vector.tensor_scalar_mul(
+            nc.scalar.mul(
                 out=v_third[:],
-                in0=u_of(chunk)[:, 2, first - 1 : first - 1 + CHUNK],
-                scalar1=conv_w[:, 2, 2:3],
+                in_=u_of(chunk)[:, 2, first - 1 : first - 1 + CHUNK],
+                mul=conv_w[:, 2, 2:3],
             )
             kept["weighted", chunk] = (v_third, v_last)
 
@@ -341,9 +342,9 @@ def tile_attention_pa_t_kernel(
             conv = conv_pool.tile([P, SPAN], F32)
             nc.scalar.activation(
                 out=conv[:],
-                in_=u_of_unit(unit, span_column(unit)),
+                in_=kept["u_bank", unit][:],
                 func=ACT.Copy,
-                scale=conv_w[:, unit % 2, TAPS - 1 : TAPS],
+                scale=last_w[:, unit % 2 : unit % 2 + 1],
             )
             kept["conv", unit] = conv
 
@@ -437,12 +438,13 @@ def tile_attention_pa_t_kernel(
             products(r)
             mean_squares(r)
             copy_v(r)
-            raise_to_power(r)
             other_tap(r - 4, 0)
             quantise_x(r + 1)
             other_tap(r - 4, 1)
+            rotated(r - 6)
             transpose_x(r + 2)
             v_products(r - 1)
+            raise_to_power(r)
             other_tap(r - 4, 2)
             normalise(r - 1)
             v_to_tokens(r - 2)
@@ -452,7 +454,6 @@ def tile_attention_pa_t_kernel(
             qk_to_tokens(r - 5)
             rotate(r - 5)
             finish_v(r - 2)
-            rotated(r - 5)
 
         for r in range(-5, 0):
             one_round(r)
@@ -474,6 +475,14 @@ def tile_attention_pa_t_kernel(
         norm_w = consts.tile([P, 2], F32)
         for grp in range(2):
             nc.vector.tensor_copy(out=norm_w[:, grp : grp + 1], in_=norm_w_bf[grp][:])
+        last_w = consts.tile([P, 2], F32)
+        for grp in range(2):
+            nc.vector.tensor_tensor(
+                out=last_w[:, grp : grp + 1],
+                in0=norm_w[:, grp : grp + 1],
+                in1=conv_w[:, grp, TAPS - 1 : TAPS],
+                op=ALU.mult,
+            )
         minus_half = consts.tile([P, SUBS * QK_HEADS], F32)
         nc.gpsimd.memset(minus_half[:], -0.5)
 
@@ -482,5 +491,5 @@ def tile_attention_pa_t_kernel(
         nc.vector.tensor_scalar_mul(
             out=sin_sb[:, :, 0:HALF], in0=sin_sb[:, :, 0:HALF], scalar1=-1.0
         )
-        for r in range(3, UNITS + 5):
+        for r in range(3, UNITS + 6):
             one_round(r)

@@ -32,7 +32,9 @@ GROUPS = 3
 QK = 2 * P
 QK_HEADS = QK // HEAD
 HALO = 8
-TENSOR_V_TAPS = (0, 1)
+TENSOR_V_TAPS = (0,)
+VECTOR_V_TAPS = (1,)
+SCALAR_V_TAPS = (2, 3)
 
 FLOPS = 2 * BATCH * SEQ * HID * GROUPS * P
 
@@ -65,6 +67,7 @@ def tile_attention_pa_t_kernel(
         norm_pool = ctx.enter_context(tc.tile_pool(name="norm_pool", bufs=4))
         u_pool = ctx.enter_context(tc.tile_pool(name="u_pool", bufs=2))
         conv_pool = ctx.enter_context(tc.tile_pool(name="conv_pool", bufs=2))
+        v_pool = ctx.enter_context(tc.tile_pool(name="v_pool", bufs=2))
         rope_pool = ctx.enter_context(tc.tile_pool(name="rope_pool", bufs=2))
         out_pool = ctx.enter_context(tc.tile_pool(name="out_pool", bufs=3))
         psum = ctx.enter_context(tc.psum_pool(name="psum", bufs=2))
@@ -274,25 +277,27 @@ def tile_attention_pa_t_kernel(
                 scale=norm_w[:, grp : grp + 1],
             )
 
-        def v_products(chunk):
+        def v_products(chunk, taps):
             if missing(chunk):
                 return
-            first = first_column(chunk)
-            v_last = conv_pool.tile([P, CHUNK], F32)
-            nc.scalar.activation(
-                out=v_last[:],
-                in_=u_of(chunk)[:, 2, first : first + CHUNK],
-                func=ACT.Identity,
-                scale=conv_w[:, 2, 3:4],
-                bias=conv_b[:, 2, :],
-            )
-            v_third = conv_pool.tile([P, CHUNK], F32)
-            nc.scalar.mul(
-                out=v_third[:],
-                in_=u_of(chunk)[:, 2, first - 1 : first - 1 + CHUNK],
-                mul=conv_w[:, 2, 2:3],
-            )
-            kept["weighted", chunk] = (v_third, v_last)
+            for tap in taps:
+                start = first_column(chunk) - (TAPS - 1 - tap)
+                v_shifted = u_of(chunk)[:, 2, start : start + CHUNK]
+                weight = conv_w[:, 2, tap : tap + 1]
+                product = v_pool.tile([P, CHUNK], F32, name="v_product_%d" % tap)
+                if tap in VECTOR_V_TAPS:
+                    nc.vector.tensor_scalar_mul(out=product[:], in0=v_shifted, scalar1=weight)
+                elif tap == TAPS - 1:
+                    nc.scalar.activation(
+                        out=product[:],
+                        in_=v_shifted,
+                        func=ACT.Identity,
+                        scale=weight,
+                        bias=conv_b[:, 2, :],
+                    )
+                else:
+                    nc.scalar.mul(out=product[:], in_=v_shifted, mul=weight)
+                kept["v_product", tap, chunk] = product
 
         def v_to_tokens(chunk):
             if missing(chunk):
@@ -309,14 +314,14 @@ def tile_attention_pa_t_kernel(
                         start=(tap == 0),
                         stop=False,
                     )
-                for weighted in kept["weighted", chunk]:
+                for tap in VECTOR_V_TAPS + SCALAR_V_TAPS:
                     nc.tensor.matmul(
                         bank[:, 0, n, :],
-                        lhsT=weighted[:, n * P : (n + 1) * P],
+                        lhsT=kept["v_product", tap, chunk][:, n * P : (n + 1) * P],
                         rhs=ident[:],
                         is_transpose=True,
                         start=False,
-                        stop=(weighted is kept["weighted", chunk][-1]),
+                        stop=(tap == TAPS - 1),
                     )
             for n in range(SUBS):
                 nc.tensor.transpose(
@@ -440,10 +445,11 @@ def tile_attention_pa_t_kernel(
             copy_v(r)
             other_tap(r - 4, 0)
             quantise_x(r + 1)
+            v_products(r - 1, VECTOR_V_TAPS)
             other_tap(r - 4, 1)
             rotated(r - 6)
             transpose_x(r + 2)
-            v_products(r - 1)
+            v_products(r - 1, SCALAR_V_TAPS)
             raise_to_power(r)
             other_tap(r - 4, 2)
             normalise(r - 1)

@@ -26,6 +26,10 @@ CHUNKS = BATCH * CHUNKS_PER_SEQ
 SPAN = 2 * CHUNK
 SPAN_TILES = SPAN // P
 SPANS_PER_SEQ = SEQ // SPAN
+HEAD_CHUNKS = 5
+TAIL_CHUNK = 29
+PACE = True
+LAST_GP = 30
 UNITS = 2 * BATCH * SPANS_PER_SEQ
 GROUP_HEADS = P // HEAD
 GROUPS = 3
@@ -33,8 +37,8 @@ QK = 2 * P
 QK_HEADS = QK // HEAD
 HALO = 8
 TENSOR_V_TAPS = (0,)
-VECTOR_V_TAPS = (1,)
-SCALAR_V_TAPS = (2, 3)
+VECTOR_V_TAPS = (1, 2)
+SCALAR_V_TAPS = (3,)
 
 FLOPS = 2 * BATCH * SEQ * HID * GROUPS * P
 
@@ -68,7 +72,7 @@ def tile_attention_pa_t_kernel(
         u_pool = ctx.enter_context(tc.tile_pool(name="u_pool", bufs=2))
         conv_pool = ctx.enter_context(tc.tile_pool(name="conv_pool", bufs=2))
         v_pool = ctx.enter_context(tc.tile_pool(name="v_pool", bufs=2))
-        rope_pool = ctx.enter_context(tc.tile_pool(name="rope_pool", bufs=2))
+        rope_pool = ctx.enter_context(tc.tile_pool(name="rope_pool", bufs=3))
         out_pool = ctx.enter_context(tc.tile_pool(name="out_pool", bufs=3))
         psum = ctx.enter_context(tc.psum_pool(name="psum", bufs=2))
 
@@ -143,9 +147,8 @@ def tile_attention_pa_t_kernel(
             for n in range(SUBS):
                 x_bank = psum.tile([P, WORD_TILES, P], F32, tag="xt")
                 transpose_words(nc, x_bank, x_raw[:, n, :], ident[:])
-                nc.scalar.copy(
-                    out=x_grouped_words[:, :, n * P : (n + 1) * P, :], in_=words_by_pass(x_bank[:])
-                )
+                copy = nc.vector.tensor_copy if n == 1 and chunk < HEAD_CHUNKS else nc.scalar.copy
+                copy(out=x_grouped_words[:, :, n * P : (n + 1) * P, :], in_=words_by_pass(x_bank[:]))
             kept["x_grouped", chunk] = x_grouped
 
         def quantise_x(chunk):
@@ -226,12 +229,21 @@ def tile_attention_pa_t_kernel(
             if missing(chunk):
                 return
             qk_normed = norm_pool.tile([P, SUBS, QK], F32)
-            nc.vector.tensor_tensor(
-                out=by_head(qk_normed[:]),
-                in0=by_head(kept["qk_bank", chunk][:]),
-                in1=kept["rstd", chunk][:].unsqueeze(2).to_broadcast([P, SUBS * QK_HEADS, HEAD]),
-                op=ALU.mult,
-            )
+            rstd = kept["rstd", chunk]
+            if chunk < TAIL_CHUNK:
+                nc.vector.tensor_tensor(
+                    out=by_head(qk_normed[:]),
+                    in0=by_head(kept["qk_bank", chunk][:]),
+                    in1=rstd[:].unsqueeze(2).to_broadcast([P, SUBS * QK_HEADS, HEAD]),
+                    op=ALU.mult,
+                )
+            else:
+                for h in range(SUBS * QK_HEADS):
+                    nc.scalar.mul(
+                        out=by_head(qk_normed[:])[:, h, :],
+                        in_=by_head(kept["qk_bank", chunk][:])[:, h, :],
+                        mul=rstd[:, h : h + 1],
+                    )
             kept["qk_normed", chunk] = qk_normed
 
         def u_of(chunk):
@@ -285,7 +297,7 @@ def tile_attention_pa_t_kernel(
                 v_shifted = u_of(chunk)[:, 2, start : start + CHUNK]
                 weight = conv_w[:, 2, tap : tap + 1]
                 product = v_pool.tile([P, CHUNK], F32, name="v_product_%d" % tap)
-                if tap in VECTOR_V_TAPS:
+                if tap in VECTOR_V_TAPS and chunk < 28:
                     nc.vector.tensor_scalar_mul(out=product[:], in0=v_shifted, scalar1=weight)
                 elif tap == TAPS - 1:
                     nc.scalar.activation(
@@ -428,7 +440,11 @@ def tile_attention_pa_t_kernel(
                 return
             straight, turned = kept["rope", unit]
             qk_out = out_pool.tile([P, SPAN_TILES, P], F32)
-            nc.vector.tensor_tensor(
+            if PACE and ("pace", unit) in kept:
+                token = v_pool.tile([P, 1], F32)
+                nc.gpsimd.tensor_copy(out=token[:], in_=kept["pace", unit][:, 0:1])
+            engine = nc.vector if unit >= LAST_GP else nc.gpsimd
+            engine.tensor_tensor(
                 out=qk_out[:].rearrange("p n (h d) -> p n h d", d=HEAD),
                 in0=straight[:],
                 in1=turned[:],
@@ -445,13 +461,15 @@ def tile_attention_pa_t_kernel(
             copy_v(r)
             other_tap(r - 4, 0)
             quantise_x(r + 1)
-            v_products(r - 1, VECTOR_V_TAPS)
             other_tap(r - 4, 1)
-            rotated(r - 6)
             transpose_x(r + 2)
             v_products(r - 1, SCALAR_V_TAPS)
-            raise_to_power(r)
+            v_products(r - 1, VECTOR_V_TAPS)
+            if not missing(r - 1):
+                kept["pace", r - 6] = kept["v_product", 1, r - 1]
             other_tap(r - 4, 2)
+            rotated(r - 6)
+            raise_to_power(r)
             normalise(r - 1)
             v_to_tokens(r - 2)
             qk_to_channels(r - 3)

@@ -26,19 +26,21 @@ CHUNKS = BATCH * CHUNKS_PER_SEQ
 SPAN = 2 * CHUNK
 SPAN_TILES = SPAN // P
 SPANS_PER_SEQ = SEQ // SPAN
-HEAD_CHUNKS = 5
+HEAD_CHUNKS = 4
 TAIL_CHUNK = 29
 PACE = True
-LAST_GP = 30
+LAST_GP = 26
 UNITS = 2 * BATCH * SPANS_PER_SEQ
 GROUP_HEADS = P // HEAD
 GROUPS = 3
 QK = 2 * P
 QK_HEADS = QK // HEAD
 HALO = 8
-TENSOR_V_TAPS = (0,)
-VECTOR_V_TAPS = (1, 2)
-SCALAR_V_TAPS = (3,)
+TENSOR, VECTOR, SCALAR = range(3)
+V_TAPS = (TENSOR, VECTOR, VECTOR, SCALAR)
+V_TAPS_HEAD = (VECTOR, VECTOR, VECTOR, SCALAR)
+V_TAPS_TAIL = (TENSOR, SCALAR, SCALAR, SCALAR)
+V_TAIL = 29
 
 FLOPS = 2 * BATCH * SEQ * HID * GROUPS * P
 
@@ -70,7 +72,7 @@ def tile_attention_pa_t_kernel(
         mx_pool = ctx.enter_context(tc.tile_pool(name="mx_pool", bufs=2))
         norm_pool = ctx.enter_context(tc.tile_pool(name="norm_pool", bufs=4))
         u_pool = ctx.enter_context(tc.tile_pool(name="u_pool", bufs=2))
-        conv_pool = ctx.enter_context(tc.tile_pool(name="conv_pool", bufs=2))
+        conv_pool = ctx.enter_context(tc.tile_pool(name="conv_pool", bufs=4))
         v_pool = ctx.enter_context(tc.tile_pool(name="v_pool", bufs=2))
         rope_pool = ctx.enter_context(tc.tile_pool(name="rope_pool", bufs=3))
         out_pool = ctx.enter_context(tc.tile_pool(name="out_pool", bufs=3))
@@ -269,11 +271,11 @@ def tile_attention_pa_t_kernel(
         def u_of_unit(unit, start):
             return u_of(unit // 2 * 2)[:, unit % 2, start : start + SPAN]
 
-        def qk_to_channels(unit):
+        def qk_to_channels(unit, tag="cl", bufs=1):
             if no_unit(unit):
                 return
             grp = unit % 2
-            u_bank = psum.tile([P, SPAN], F32, tag="cl", bufs=1)
+            u_bank = psum.tile([P, SPAN], F32, tag=tag, bufs=bufs)
             for tile in range(SPAN_TILES):
                 chunk, n = unit // 2 * 2 + tile // SUBS, tile % SUBS
                 nc.tensor.transpose(
@@ -289,15 +291,19 @@ def tile_attention_pa_t_kernel(
                 scale=norm_w[:, grp : grp + 1],
             )
 
-        def v_products(chunk, taps):
+        def v_taps(chunk, engine):
+            plan = V_TAPS_HEAD if chunk < HEAD_CHUNKS else V_TAPS_TAIL if chunk >= V_TAIL else V_TAPS
+            return [tap for tap in range(TAPS) if plan[tap] == engine]
+
+        def v_products(chunk, engine):
             if missing(chunk):
                 return
-            for tap in taps:
+            for tap in v_taps(chunk, engine):
                 start = first_column(chunk) - (TAPS - 1 - tap)
                 v_shifted = u_of(chunk)[:, 2, start : start + CHUNK]
                 weight = conv_w[:, 2, tap : tap + 1]
                 product = v_pool.tile([P, CHUNK], F32, name="v_product_%d" % tap)
-                if tap in VECTOR_V_TAPS and chunk < 28:
+                if engine == VECTOR:
                     nc.vector.tensor_scalar_mul(out=product[:], in0=v_shifted, scalar1=weight)
                 elif tap == TAPS - 1:
                     nc.scalar.activation(
@@ -312,27 +318,28 @@ def tile_attention_pa_t_kernel(
                 kept["v_product", tap, chunk] = product
 
         def v_to_tokens(chunk):
+            vtag = "xt" if chunk >= 29 else "zt"
             if missing(chunk):
                 return
             first = first_column(chunk)
-            bank = psum.tile([P, 2, SUBS, P], F32, tag="zt")
+            bank = psum.tile([P, 2, SUBS, P], F32, tag=vtag)
             for n in range(SUBS):
-                for tap in TENSOR_V_TAPS:
+                for tap in v_taps(chunk, TENSOR):
                     start = first + n * P - (TAPS - 1 - tap)
                     nc.tensor.matmul(
                         bank[:, 0, n, :],
                         lhsT=u_of(chunk)[:, 2, start : start + P],
-                        rhs=v_diag[:, tap, :],
+                        rhs=v_diag[:],
                         start=(tap == 0),
                         stop=False,
                     )
-                for tap in VECTOR_V_TAPS + SCALAR_V_TAPS:
+                for tap in sorted(v_taps(chunk, VECTOR) + v_taps(chunk, SCALAR)):
                     nc.tensor.matmul(
                         bank[:, 0, n, :],
                         lhsT=kept["v_product", tap, chunk][:, n * P : (n + 1) * P],
                         rhs=ident[:],
                         is_transpose=True,
-                        start=False,
+                        start=(tap == 0),
                         stop=(tap == TAPS - 1),
                     )
             for n in range(SUBS):
@@ -415,7 +422,7 @@ def tile_attention_pa_t_kernel(
                 )
             kept["z_bank", unit] = z_bank
 
-        def rotate(unit):
+        def rotate(unit, parts=(0, 1)):
             if no_unit(unit):
                 return
             z = kept["z_bank", unit][:].rearrange("p n (h d) -> p n h d", d=HEAD)
@@ -423,8 +430,12 @@ def tile_attention_pa_t_kernel(
             table_shape = [P, SPAN_TILES, GROUP_HEADS, HEAD]
             cos_b = cos_sb[:, j : j + SPAN_TILES, :].unsqueeze(2).to_broadcast(table_shape)
             sin_b = sin_sb[:, j : j + SPAN_TILES, :].unsqueeze(2).to_broadcast(table_shape)
-            straight = rope_pool.tile(table_shape, F32)
-            nc.vector.tensor_tensor(out=straight[:], in0=z, in1=cos_b, op=ALU.mult)
+            if 0 in parts:
+                straight = rope_pool.tile(table_shape, F32)
+                kept["straight", unit] = straight
+                nc.vector.tensor_tensor(out=straight[:], in0=z, in1=cos_b, op=ALU.mult)
+            if 1 not in parts:
+                return
             turned = rope_pool.tile(table_shape, F32)
             by_half = "p n h (s d) -> p n h s d"
             nc.vector.tensor_tensor(
@@ -433,7 +444,7 @@ def tile_attention_pa_t_kernel(
                 in1=sin_b.rearrange(by_half, s=2),
                 op=ALU.mult,
             )
-            kept["rope", unit] = (straight, turned)
+            kept["rope", unit] = (kept["straight", unit], turned)
 
         def rotated(unit):
             if no_unit(unit):
@@ -443,7 +454,7 @@ def tile_attention_pa_t_kernel(
             if PACE and ("pace", unit) in kept:
                 token = v_pool.tile([P, 1], F32)
                 nc.gpsimd.tensor_copy(out=token[:], in_=kept["pace", unit][:, 0:1])
-            engine = nc.vector if unit >= LAST_GP else nc.gpsimd
+            engine = nc.vector if (25 <= unit <= 27 or unit == 31) else nc.gpsimd
             engine.tensor_tensor(
                 out=qk_out[:].rearrange("p n (h d) -> p n h d", d=HEAD),
                 in0=straight[:],
@@ -463,10 +474,10 @@ def tile_attention_pa_t_kernel(
             quantise_x(r + 1)
             other_tap(r - 4, 1)
             transpose_x(r + 2)
-            v_products(r - 1, SCALAR_V_TAPS)
-            v_products(r - 1, VECTOR_V_TAPS)
+            v_products(r - 1, SCALAR)
+            v_products(r - 1, VECTOR)
             if not missing(r - 1):
-                kept["pace", r - 6] = kept["v_product", 1, r - 1]
+                kept["pace", r - 6] = kept["v_product", 2, r - 1]
             other_tap(r - 4, 2)
             rotated(r - 6)
             raise_to_power(r)
@@ -491,11 +502,8 @@ def tile_attention_pa_t_kernel(
         nc.vector.tensor_copy(out=conv_w[:], in_=conv_w_bf[:])
         conv_b = consts.tile([P, GROUPS, 1], F32)
         nc.vector.tensor_copy(out=conv_b[:], in_=conv_b_bf[:])
-        v_diag = consts.tile([P, len(TENSOR_V_TAPS), P], F32)
-        for tap in TENSOR_V_TAPS:
-            nc.vector.tensor_scalar_mul(
-                out=v_diag[:, tap, :], in0=ident[:], scalar1=conv_w[:, 2, tap : tap + 1]
-            )
+        v_diag = consts.tile([P, P], F32)
+        nc.vector.tensor_scalar_mul(out=v_diag[:], in0=ident[:], scalar1=conv_w[:, 2, 0:1])
         norm_w = consts.tile([P, 2], F32)
         for grp in range(2):
             nc.vector.tensor_copy(out=norm_w[:, grp : grp + 1], in_=norm_w_bf[grp][:])
@@ -515,5 +523,73 @@ def tile_attention_pa_t_kernel(
         nc.vector.tensor_scalar_mul(
             out=sin_sb[:, :, 0:HALF], in0=sin_sb[:, :, 0:HALF], scalar1=-1.0
         )
-        for r in range(3, UNITS + 6):
+        def rotate1(u):
+            rotate(u, (0,))
+        def rotate2(u):
+            rotate(u, (1,))
+        for r in range(3, 31):
             one_round(r)
+        products(31)
+        qk_to_tokens(26)
+        copy_v(31)
+        mean_squares(31)
+        raise_to_power(31)
+        other_tap(27, 0)
+        rotated(25)
+        qk_to_channels(28)
+        last_tap(28)
+        v_to_tokens(29)
+        other_tap(27, 1)
+        rotate1(26)
+        normalise(30)
+        other_tap(27, 2)
+        gate(27)
+        qk_to_channels(29)
+        qk_to_tokens(27)
+        last_tap(29)
+        rotate2(26)
+        other_tap(28, 0)
+        finish_v(29)
+        other_tap(28, 1)
+        rotated(26)
+        normalise(31)
+        rotate1(27)
+        other_tap(28, 2)
+        qk_to_channels(30, "qk", 3)
+        qk_to_channels(31, "qk", 3)
+        rotate2(27)
+        gate(28)
+        last_tap(30)
+        last_tap(31)
+        other_tap(29, 0)
+        v_products(30, SCALAR)
+        qk_to_tokens(28)
+        other_tap(29, 1)
+        v_to_tokens(30)
+        rotate1(28)
+        other_tap(29, 2)
+        gate(29)
+        rotate2(28)
+        other_tap(30, 0)
+        other_tap(31, 0)
+        v_products(31, SCALAR)
+        qk_to_tokens(29)
+        rotated(27)
+        other_tap(30, 1)
+        other_tap(31, 1)
+        other_tap(30, 2)
+        other_tap(31, 2)
+        gate(30)
+        gate(31)
+        v_to_tokens(31)
+        qk_to_tokens(30)
+        rotate(29)
+        rotated(28)
+        finish_v(30)
+        qk_to_tokens(31)
+        rotate(30)
+        rotated(29)
+        finish_v(31)
+        rotate(31)
+        rotated(30)
+        rotated(31)

@@ -122,7 +122,7 @@ def tile_attention_pa_t_kernel(
                     in_=w_grouped[:, g, 4 * lo : 4 * hi],
                 )
 
-        kept = {}
+        kept = {"paced": set()}
 
         def missing(chunk):
             return not 0 <= chunk < CHUNKS
@@ -302,19 +302,26 @@ def tile_attention_pa_t_kernel(
                 start = first_column(chunk) - (TAPS - 1 - tap)
                 v_shifted = u_of(chunk)[:, 2, start : start + CHUNK]
                 weight = conv_w[:, 2, tap : tap + 1]
-                product = v_pool.tile([P, CHUNK], F32, name="v_product_%d" % tap)
+                rope = kept.get(("rope", chunk - 5))
                 if engine == VECTOR:
-                    nc.vector.tensor_scalar_mul(out=product[:], in0=v_shifted, scalar1=weight)
+                    if rope and tap > 0:
+                        product = rope[tap - 1][:, SPAN : SPAN + CHUNK]
+                        kept["paced"].add(chunk - 5)
+                    else:
+                        product = v_pool.tile([P, CHUNK], F32, name="v_product_%d" % tap)[:]
+                    nc.vector.tensor_scalar_mul(out=product, in0=v_shifted, scalar1=weight)
                 elif tap == TAPS - 1:
+                    product = v_pool.tile([P, CHUNK], F32, name="v_product_%d" % tap)[:]
                     nc.scalar.activation(
-                        out=product[:],
+                        out=product,
                         in_=v_shifted,
                         func=ACT.Identity,
                         scale=weight,
                         bias=conv_b[:, 2, :],
                     )
                 else:
-                    nc.scalar.mul(out=product[:], in_=v_shifted, mul=weight)
+                    product = v_pool.tile([P, CHUNK], F32, name="v_product_%d" % tap)[:]
+                    nc.scalar.mul(out=product, in_=v_shifted, mul=weight)
                 kept["v_product", tap, chunk] = product
 
         def v_to_tokens(chunk):
@@ -431,15 +438,15 @@ def tile_attention_pa_t_kernel(
             cos_b = cos_sb[:, j : j + SPAN_TILES, :].unsqueeze(2).to_broadcast(table_shape)
             sin_b = sin_sb[:, j : j + SPAN_TILES, :].unsqueeze(2).to_broadcast(table_shape)
             if 0 in parts:
-                straight = rope_pool.tile(table_shape, F32)
+                straight = rope_pool.tile([P, SPAN + CHUNK], F32)
                 kept["straight", unit] = straight
-                nc.vector.tensor_tensor(out=straight[:], in0=z, in1=cos_b, op=ALU.mult)
+                nc.vector.tensor_tensor(out=straight[:, 0:SPAN].rearrange("p (n h d) -> p n h d", h=GROUP_HEADS, d=HEAD), in0=z, in1=cos_b, op=ALU.mult)
             if 1 not in parts:
                 return
-            turned = rope_pool.tile(table_shape, F32)
+            turned = rope_pool.tile([P, SPAN + CHUNK], F32)
             by_half = "p n h (s d) -> p n h s d"
             nc.vector.tensor_tensor(
-                out=turned[:].rearrange(by_half, s=2),
+                out=turned[:, 0:SPAN].rearrange("p (n h d) -> p n h d", h=GROUP_HEADS, d=HEAD).rearrange(by_half, s=2),
                 in0=z.rearrange(by_half, s=2)[:, :, :, ::-1, :],
                 in1=sin_b.rearrange(by_half, s=2),
                 op=ALU.mult,
@@ -450,19 +457,17 @@ def tile_attention_pa_t_kernel(
             if no_unit(unit):
                 return
             straight, turned = kept["rope", unit]
-            qk_out = out_pool.tile([P, SPAN_TILES, P], F32)
-            if PACE and ("pace", unit) in kept:
-                token = v_pool.tile([P, 1], F32)
-                nc.gpsimd.tensor_copy(out=token[:], in_=kept["pace", unit][:, 0:1])
+            qk_out = out_pool.tile([P, SPAN + 1], F32)
+            width = SPAN + 1 if unit in kept["paced"] else SPAN
             engine = nc.vector if (25 <= unit <= 27 or unit == 31) else nc.gpsimd
             engine.tensor_tensor(
-                out=qk_out[:].rearrange("p n (h d) -> p n h d", d=HEAD),
-                in0=straight[:],
-                in1=turned[:],
+                out=qk_out[:, 0:width],
+                in0=straight[:, 0:width],
+                in1=turned[:, 0:width],
                 op=ALU.add,
             )
             nc.sync.dma_start(
-                out=rows_of(out_rows[unit % 2], unit // 2 * SPAN, SPAN_TILES), in_=qk_out[:]
+                out=rows_of(out_rows[unit % 2], unit // 2 * SPAN, SPAN_TILES), in_=qk_out[:, 0:SPAN].rearrange("p (n c) -> p n c", c=P)
             )
 
         def one_round(r):
@@ -476,19 +481,17 @@ def tile_attention_pa_t_kernel(
             transpose_x(r + 2)
             v_products(r - 1, SCALAR)
             v_products(r - 1, VECTOR)
-            if not missing(r - 1):
-                kept["pace", r - 6] = kept["v_product", 2, r - 1]
             other_tap(r - 4, 2)
             rotated(r - 6)
             raise_to_power(r)
-            normalise(r - 1)
             v_to_tokens(r - 2)
             qk_to_channels(r - 3)
             last_tap(r - 3)
             gate(r - 4)
             qk_to_tokens(r - 5)
-            rotate(r - 5)
             finish_v(r - 2)
+            rotate(r - 5)
+            normalise(r - 1)
 
         for r in range(-5, 0):
             one_round(r)

from contextlib import ExitStack

import concourse.mybir as mybir
from concourse.masks import make_identity

F32 = mybir.dt.float32
BF16 = mybir.dt.bfloat16
U32 = mybir.dt.uint32
U8 = mybir.dt.uint8
FP8X4 = mybir.dt.float8_e4m3fn_x4
ALU = mybir.AluOpType
ACT = mybir.ActivationFunctionType

P = 128
BATCH, SEQ, HID = 4, 2048, 1024
HEAD = 64
HALF = HEAD // 2
TAPS = 4
EPS = 1e-5
PASSES = HID // (4 * P)
WORD_TILES = HID // (2 * P)
CHUNK = 256
SUBS = CHUNK // P
CHUNKS_PER_SEQ = SEQ // CHUNK
CHUNKS = BATCH * CHUNKS_PER_SEQ
SPAN = 2 * CHUNK
SPAN_TILES = SPAN // P
SPANS_PER_SEQ = SEQ // SPAN
HEAD_CHUNKS = 4
TAIL_CHUNK = 29
PACE = True
LAST_GP = 26
UNITS = 2 * BATCH * SPANS_PER_SEQ
GROUP_HEADS = P // HEAD
GROUPS = 3
QK = 2 * P
QK_HEADS = QK // HEAD
HALO = 8
TENSOR, VECTOR, SCALAR = range(3)
V_TAPS = (TENSOR, VECTOR, VECTOR, SCALAR)
V_TAPS_HEAD = (VECTOR, VECTOR, VECTOR, SCALAR)
V_TAPS_TAIL = (TENSOR, SCALAR, SCALAR, SCALAR)
V_TAIL = 29

FLOPS = 2 * BATCH * SEQ * HID * GROUPS * P


def transpose_words(nc, bank, rows, ident):
    words = rows.bitcast(F32)
    for w in range(WORD_TILES):
        g, u = divmod(w, 2)
        nc.tensor.transpose(
            bank[:, w, :], words[:, 2 * P * g + u : 2 * P * (g + 1) : 2], ident
        )


def words_by_pass(bank):
    return bank.rearrange("p (g u) r -> p g r u", u=2)


def tile_attention_pa_t_kernel(
    tc, x, cos, sin, q_w, k_w, v_w, q_norm_w, k_norm_w, canon_w, canon_bias, out_0, out_1, out_2
):
    nc = tc.nc
    x_rows = x.flatten_outer_dims()
    out_rows = [o.rearrange("b s h d -> (b s) (h d)") for o in (out_0, out_1, out_2)]

    with ExitStack() as ctx:
        ctx.enter_context(tc.manual_schedule())
        consts = ctx.enter_context(tc.tile_pool(name="consts", bufs=1))
        x_pool = ctx.enter_context(tc.tile_pool(name="x_pool", bufs=4))
        mx_pool = ctx.enter_context(tc.tile_pool(name="mx_pool", bufs=2))
        norm_pool = ctx.enter_context(tc.tile_pool(name="norm_pool", bufs=4))
        u_pool = ctx.enter_context(tc.tile_pool(name="u_pool", bufs=2))
        conv_pool = ctx.enter_context(tc.tile_pool(name="conv_pool", bufs=4))
        v_pool = ctx.enter_context(tc.tile_pool(name="v_pool", bufs=2))
        rope_pool = ctx.enter_context(tc.tile_pool(name="rope_pool", bufs=3))
        out_pool = ctx.enter_context(tc.tile_pool(name="out_pool", bufs=3))
        psum = ctx.enter_context(tc.psum_pool(name="psum", bufs=2))

        warm = consts.tile([P, 1], F32)
        nc.vector.memset(warm[:], 0.0)
        warmed = consts.tile([P, 1], F32)
        nc.scalar.activation(out=warmed[:], in_=warm[:], func=ACT.Silu)

        ident = consts.tile([P, P], F32)
        make_identity(nc, ident[:])

        w_raw = consts.tile([P, GROUPS, HID], BF16)
        for grp, w in enumerate((q_w, k_w, v_w)):
            nc.sync.dma_start(out=w_raw[:, grp, :], in_=w)
        conv_w_bf = consts.tile([P, GROUPS, TAPS], BF16)
        nc.scalar.dma_start(out=conv_w_bf[:], in_=canon_w.rearrange("(g c) j -> c g j", g=GROUPS))
        conv_b_bf = consts.tile([P, GROUPS, 1], BF16)
        nc.scalar.dma_start(
            out=conv_b_bf[:], in_=canon_bias.rearrange("(g c o) -> c g o", g=GROUPS, o=1)
        )
        norm_w_bf = []
        for w in (q_norm_w, k_norm_w):
            repeated = consts.tile([P, 1], BF16, name="norm_w_bf%d" % len(norm_w_bf))
            for head in range(P // HEAD):
                nc.gpsimd.dma_start(
                    out=repeated[head * HEAD : (head + 1) * HEAD, :],
                    in_=w.rearrange("(d o) -> d o", o=1),
                )
            norm_w_bf.append(repeated)
        w_grouped = consts.tile([P, PASSES, GROUPS * P * 4], BF16, align_bytes=64)
        w_grouped_words = w_grouped[:].bitcast(F32).rearrange("p g (m u) -> p g m u", u=2)
        for grp in range(GROUPS):
            w_bank = psum.tile([P, WORD_TILES, P], F32, tag="xt")
            transpose_words(nc, w_bank, w_raw[:, grp, :], ident[:])
            nc.vector.tensor_copy(
                out=w_grouped_words[:, :, grp * P : (grp + 1) * P, :], in_=words_by_pass(w_bank[:])
            )
        w_codes = consts.tile([P, PASSES, GROUPS * P], U32, align_bytes=64)
        w_scales = consts.tile([P, PASSES, GROUPS * P], U8, align_bytes=64)
        for g in range(PASSES):
            for lo, hi in ((0, QK), (QK, QK + P)):
                nc.vector.quantize_mx(
                    out=w_codes[:, g, lo:hi].bitcast(FP8X4),
                    scales=w_scales[:, g, lo:hi],
                    in_=w_grouped[:, g, 4 * lo : 4 * hi],
                )

        kept = {"paced": set()}

        def missing(chunk):
            return not 0 <= chunk < CHUNKS

        def first_column(chunk):
            return HALO + (chunk % CHUNKS_PER_SEQ) * CHUNK

        def load_x(chunk):
            if missing(chunk):
                return
            x_raw = x_pool.tile([P, SUBS, HID], BF16)
            nc.sync.dma_start(
                out=x_raw[:],
                in_=x_rows[chunk * CHUNK : (chunk + 1) * CHUNK, :].rearrange("(n p) k -> p n k", p=P),
            )
            kept["x_raw", chunk] = x_raw

        def transpose_x(chunk):
            if missing(chunk):
                return
            x_raw = kept["x_raw", chunk]
            x_grouped = mx_pool.tile([P, PASSES, CHUNK * 4], BF16, align_bytes=64)
            x_grouped_words = x_grouped[:].bitcast(F32).rearrange("p g (t u) -> p g t u", u=2)
            for n in range(SUBS):
                x_bank = psum.tile([P, WORD_TILES, P], F32, tag="xt")
                transpose_words(nc, x_bank, x_raw[:, n, :], ident[:])
                copy = nc.vector.tensor_copy if n == 1 and chunk < HEAD_CHUNKS else nc.scalar.copy
                copy(out=x_grouped_words[:, :, n * P : (n + 1) * P, :], in_=words_by_pass(x_bank[:]))
            kept["x_grouped", chunk] = x_grouped

        def quantise_x(chunk):
            if missing(chunk):
                return
            x_codes = mx_pool.tile([P, PASSES, CHUNK], U32, align_bytes=64)
            x_scales = mx_pool.tile([P, PASSES, CHUNK], U8, align_bytes=64)
            nc.vector.quantize_mx(
                out=x_codes[:].rearrange("p g t -> p (g t)").bitcast(FP8X4),
                scales=x_scales[:].rearrange("p g t -> p (g t)"),
                in_=kept["x_grouped", chunk][:].rearrange("p g c -> p (g c)"),
            )
            kept["x_codes", chunk] = x_codes
            kept["x_scales", chunk] = x_scales

        def products(chunk):
            if missing(chunk):
                return
            x_codes = kept["x_codes", chunk]
            x_scales = kept["x_scales", chunk]
            qk_bank = psum.tile([P, SUBS, QK], F32, tag="qk", bufs=3)
            for n in range(SUBS):
                for g in range(PASSES):
                    nc.tensor.matmul_mx(
                        out=qk_bank[:, n, :],
                        lhsT=x_codes[:, g, n * P : (n + 1) * P].bitcast(FP8X4),
                        lhsT_scale=x_scales[:, g, n * P : (n + 1) * P],
                        rhs=w_codes[:, g, 0:QK].bitcast(FP8X4),
                        rhs_scale=w_scales[:, g, 0:QK],
                        start=(g == 0),
                        stop=(g == PASSES - 1),
                    )
            kept["qk_bank", chunk] = qk_bank
            v_bank = psum.tile([P, CHUNK], F32, tag="cl", bufs=1)
            for g in range(PASSES):
                nc.tensor.matmul_mx(
                    out=v_bank[:],
                    lhsT=w_codes[:, g, QK : QK + P].bitcast(FP8X4),
                    lhsT_scale=w_scales[:, g, QK : QK + P],
                    rhs=x_codes[:, g, :].bitcast(FP8X4),
                    rhs_scale=x_scales[:, g, :],
                    start=(g == 0),
                    stop=(g == PASSES - 1),
                )
            kept["v_bank", chunk] = v_bank

        def by_head(qk):
            return qk.rearrange("p n (h d) -> p (n h) d", d=HEAD)

        def mean_squares(chunk):
            if missing(chunk):
                return
            qk_heads = by_head(kept["qk_bank", chunk][:])
            squares = norm_pool.tile([P, SUBS * QK_HEADS, HEAD], F32)
            mean_sq = norm_pool.tile([P, SUBS * QK_HEADS], F32)
            for h in range(SUBS * QK_HEADS):
                nc.scalar.activation(
                    out=squares[:, h, :],
                    in_=qk_heads[:, h, :],
                    func=ACT.Square,
                    scale=0.125,
                    accum_out=mean_sq[:, h : h + 1],
                )
            kept["mean_sq", chunk] = mean_sq

        def raise_to_power(chunk):
            if missing(chunk):
                return
            shifted = norm_pool.tile([P, SUBS * QK_HEADS], F32)
            nc.scalar.activation(
                out=shifted[:], in_=kept["mean_sq", chunk][:], func=ACT.Copy, bias=EPS
            )
            rstd = norm_pool.tile([P, SUBS * QK_HEADS], F32)
            nc.gpsimd.tensor_tensor(out=rstd[:], in0=shifted[:], in1=minus_half[:], op=ALU.pow)
            kept["rstd", chunk] = rstd

        def normalise(chunk):
            if missing(chunk):
                return
            qk_normed = norm_pool.tile([P, SUBS, QK], F32)
            rstd = kept["rstd", chunk]
            if chunk < TAIL_CHUNK:
                nc.vector.tensor_tensor(
                    out=by_head(qk_normed[:]),
                    in0=by_head(kept["qk_bank", chunk][:]),
                    in1=rstd[:].unsqueeze(2).to_broadcast([P, SUBS * QK_HEADS, HEAD]),
                    op=ALU.mult,
                )
            else:
                for h in range(SUBS * QK_HEADS):
                    nc.scalar.mul(
                        out=by_head(qk_normed[:])[:, h, :],
                        in_=by_head(kept["qk_bank", chunk][:])[:, h, :],
                        mul=rstd[:, h : h + 1],
                    )
            kept["qk_normed", chunk] = qk_normed

        def u_of(chunk):
            seq = chunk // CHUNKS_PER_SEQ
            if ("u", seq) not in kept:
                u = u_pool.tile([P, GROUPS, HALO + SEQ], F32)
                nc.gpsimd.memset(u[:, :, 0:HALO], 0.0)
                kept["u", seq] = u
            return kept["u", seq]

        def copy_v(chunk):
            if missing(chunk):
                return
            first = first_column(chunk)
            nc.scalar.copy(out=u_of(chunk)[:, 2, first : first + CHUNK], in_=kept["v_bank", chunk][:])

        def no_unit(unit):
            return not 0 <= unit < UNITS

        def span_column(unit):
            return HALO + (unit // 2 % SPANS_PER_SEQ) * SPAN

        def u_of_unit(unit, start):
            return u_of(unit // 2 * 2)[:, unit % 2, start : start + SPAN]

        def qk_to_channels(unit, tag="cl", bufs=1):
            if no_unit(unit):
                return
            grp = unit % 2
            u_bank = psum.tile([P, SPAN], F32, tag=tag, bufs=bufs)
            for tile in range(SPAN_TILES):
                chunk, n = unit // 2 * 2 + tile // SUBS, tile % SUBS
                nc.tensor.transpose(
                    u_bank[:, tile * P : (tile + 1) * P],
                    kept["qk_normed", chunk][:, n, grp * P : (grp + 1) * P],
                    ident[:],
                )
            kept["u_bank", unit] = u_bank
            nc.scalar.activation(
                out=u_of_unit(unit, span_column(unit)),
                in_=u_bank[:],
                func=ACT.Copy,
                scale=norm_w[:, grp : grp + 1],
            )

        def v_taps(chunk, engine):
            plan = V_TAPS_HEAD if chunk < HEAD_CHUNKS else V_TAPS_TAIL if chunk >= V_TAIL else V_TAPS
            return [tap for tap in range(TAPS) if plan[tap] == engine]

        def v_products(chunk, engine):
            if missing(chunk):
                return
            for tap in v_taps(chunk, engine):
                start = first_column(chunk) - (TAPS - 1 - tap)
                v_shifted = u_of(chunk)[:, 2, start : start + CHUNK]
                weight = conv_w[:, 2, tap : tap + 1]
                rope = kept.get(("rope", chunk - 5))
                if engine == VECTOR:
                    if rope and tap > 0:
                        product = rope[tap - 1][:, SPAN : SPAN + CHUNK]
                        kept["paced"].add(chunk - 5)
                    else:
                        product = v_pool.tile([P, CHUNK], F32, name="v_product_%d" % tap)[:]
                    nc.vector.tensor_scalar_mul(out=product, in0=v_shifted, scalar1=weight)
                elif tap == TAPS - 1:
                    product = v_pool.tile([P, CHUNK], F32, name="v_product_%d" % tap)[:]
                    nc.scalar.activation(
                        out=product,
                        in_=v_shifted,
                        func=ACT.Identity,
                        scale=weight,
                        bias=conv_b[:, 2, :],
                    )
                else:
                    product = v_pool.tile([P, CHUNK], F32, name="v_product_%d" % tap)[:]
                    nc.scalar.mul(out=product, in_=v_shifted, mul=weight)
                kept["v_product", tap, chunk] = product

        def v_to_tokens(chunk):
            vtag = "xt" if chunk >= 29 else "zt"
            if missing(chunk):
                return
            first = first_column(chunk)
            bank = psum.tile([P, 2, SUBS, P], F32, tag=vtag)
            for n in range(SUBS):
                for tap in v_taps(chunk, TENSOR):
                    start = first + n * P - (TAPS - 1 - tap)
                    nc.tensor.matmul(
                        bank[:, 0, n, :],
                        lhsT=u_of(chunk)[:, 2, start : start + P],
                        rhs=v_diag[:],
                        start=(tap == 0),
                        stop=False,
                    )
                for tap in sorted(v_taps(chunk, VECTOR) + v_taps(chunk, SCALAR)):
                    nc.tensor.matmul(
                        bank[:, 0, n, :],
                        lhsT=kept["v_product", tap, chunk][:, n * P : (n + 1) * P],
                        rhs=ident[:],
                        is_transpose=True,
                        start=(tap == 0),
                        stop=(tap == TAPS - 1),
                    )
            for n in range(SUBS):
                nc.tensor.transpose(
                    bank[:, 1, n, :], u_of(chunk)[:, 2, first + n * P : first + (n + 1) * P], ident[:]
                )
            kept["v_tokens", chunk] = bank
            gated_v = out_pool.tile([P, SUBS, P], F32)
            nc.scalar.activation(out=gated_v[:], in_=bank[:, 0], func=ACT.Silu)
            kept["gated_v", chunk] = gated_v

        def finish_v(chunk):
            if missing(chunk):
                return
            v_out = out_pool.tile([P, SUBS, P], F32)
            nc.vector.tensor_tensor(
                out=v_out[:], in0=kept["v_tokens", chunk][:, 1], in1=kept["gated_v", chunk][:], op=ALU.add
            )
            nc.sync.dma_start(out=rows_of(out_rows[2], chunk * CHUNK, SUBS), in_=v_out[:])

        def last_tap(unit):
            if no_unit(unit):
                return
            conv = conv_pool.tile([P, SPAN], F32)
            nc.scalar.activation(
                out=conv[:],
                in_=kept["u_bank", unit][:],
                func=ACT.Copy,
                scale=last_w[:, unit % 2 : unit % 2 + 1],
            )
            kept["conv", unit] = conv

        def other_tap(unit, tap):
            if no_unit(unit):
                return
            conv = kept["conv", unit]
            nc.vector.scalar_tensor_tensor(
                out=conv[:],
                in0=u_of_unit(unit, span_column(unit) - (TAPS - 1 - tap)),
                scalar=conv_w[:, unit % 2, tap : tap + 1],
                in1=conv[:],
                op0=ALU.mult,
                op1=ALU.add,
            )

        def gate(unit):
            if no_unit(unit):
                return
            gated = conv_pool.tile([P, SPAN], F32)
            nc.scalar.activation(
                out=gated[:], in_=kept["conv", unit][:], func=ACT.Silu, bias=conv_b[:, unit % 2, :]
            )
            kept["gated", unit] = gated

        def rows_of(out, first, tiles):
            return out[first : first + tiles * P, :].rearrange("(n p) c -> p n c", p=P)

        def qk_to_tokens(unit):
            if no_unit(unit):
                return
            z_bank = psum.tile([P, SPAN_TILES, P], F32, tag="zt")
            u = u_of_unit(unit, span_column(unit))
            for tile in range(SPAN_TILES):
                tokens = slice(tile * P, (tile + 1) * P)
                nc.tensor.matmul(
                    z_bank[:, tile, :],
                    lhsT=kept["gated", unit][:, tokens],
                    rhs=ident[:],
                    is_transpose=True,
                    start=True,
                    stop=False,
                )
                nc.tensor.matmul(
                    z_bank[:, tile, :],
                    lhsT=u[:, tokens],
                    rhs=ident[:],
                    is_transpose=True,
                    start=False,
                    stop=True,
                )
            kept["z_bank", unit] = z_bank

        def rotate(unit, parts=(0, 1)):
            if no_unit(unit):
                return
            z = kept["z_bank", unit][:].rearrange("p n (h d) -> p n h d", d=HEAD)
            j = (unit // 2 % SPANS_PER_SEQ) * SPAN_TILES
            table_shape = [P, SPAN_TILES, GROUP_HEADS, HEAD]
            cos_b = cos_sb[:, j : j + SPAN_TILES, :].unsqueeze(2).to_broadcast(table_shape)
            sin_b = sin_sb[:, j : j + SPAN_TILES, :].unsqueeze(2).to_broadcast(table_shape)
            if 0 in parts:
                straight = rope_pool.tile([P, SPAN + CHUNK], F32)
                kept["straight", unit] = straight
                nc.vector.tensor_tensor(out=straight[:, 0:SPAN].rearrange("p (n h d) -> p n h d", h=GROUP_HEADS, d=HEAD), in0=z, in1=cos_b, op=ALU.mult)
            if 1 not in parts:
                return
            turned = rope_pool.tile([P, SPAN + CHUNK], F32)
            by_half = "p n h (s d) -> p n h s d"
            nc.vector.tensor_tensor(
                out=turned[:, 0:SPAN].rearrange("p (n h d) -> p n h d", h=GROUP_HEADS, d=HEAD).rearrange(by_half, s=2),
                in0=z.rearrange(by_half, s=2)[:, :, :, ::-1, :],
                in1=sin_b.rearrange(by_half, s=2),
                op=ALU.mult,
            )
            kept["rope", unit] = (kept["straight", unit], turned)

        def rotated(unit):
            if no_unit(unit):
                return
            straight, turned = kept["rope", unit]
            qk_out = out_pool.tile([P, SPAN + 1], F32)
            width = SPAN + 1 if unit in kept["paced"] else SPAN
            engine = nc.vector if (25 <= unit <= 27 or unit == 31) else nc.gpsimd
            engine.tensor_tensor(
                out=qk_out[:, 0:width],
                in0=straight[:, 0:width],
                in1=turned[:, 0:width],
                op=ALU.add,
            )
            nc.sync.dma_start(
                out=rows_of(out_rows[unit % 2], unit // 2 * SPAN, SPAN_TILES), in_=qk_out[:, 0:SPAN].rearrange("p (n c) -> p n c", c=P)
            )

        def one_round(r):
            load_x(r + 5)
            products(r)
            mean_squares(r)
            copy_v(r)
            other_tap(r - 4, 0)
            quantise_x(r + 1)
            other_tap(r - 4, 1)
            transpose_x(r + 2)
            v_products(r - 1, SCALAR)
            v_products(r - 1, VECTOR)
            other_tap(r - 4, 2)
            rotated(r - 6)
            raise_to_power(r)
            v_to_tokens(r - 2)
            qk_to_channels(r - 3)
            last_tap(r - 3)
            gate(r - 4)
            qk_to_tokens(r - 5)
            finish_v(r - 2)
            rotate(r - 5)
            normalise(r - 1)

        for r in range(-5, 0):
            one_round(r)

        cos_sb = consts.tile([P, SEQ // P, HEAD], BF16)
        nc.scalar.dma_start(out=cos_sb[:], in_=cos.rearrange("(j p) d -> p j d", p=P))
        sin_sb = consts.tile([P, SEQ // P, HEAD], BF16)
        nc.scalar.dma_start(out=sin_sb[:], in_=sin.rearrange("(j p) d -> p j d", p=P))

        conv_w = consts.tile([P, GROUPS, TAPS], F32)
        nc.vector.tensor_copy(out=conv_w[:], in_=conv_w_bf[:])
        conv_b = consts.tile([P, GROUPS, 1], F32)
        nc.vector.tensor_copy(out=conv_b[:], in_=conv_b_bf[:])
        v_diag = consts.tile([P, P], F32)
        nc.vector.tensor_scalar_mul(out=v_diag[:], in0=ident[:], scalar1=conv_w[:, 2, 0:1])
        norm_w = consts.tile([P, 2], F32)
        for grp in range(2):
            nc.vector.tensor_copy(out=norm_w[:, grp : grp + 1], in_=norm_w_bf[grp][:])
        last_w = consts.tile([P, 2], F32)
        for grp in range(2):
            nc.vector.tensor_tensor(
                out=last_w[:, grp : grp + 1],
                in0=norm_w[:, grp : grp + 1],
                in1=conv_w[:, grp, TAPS - 1 : TAPS],
                op=ALU.mult,
            )
        minus_half = consts.tile([P, SUBS * QK_HEADS], F32)
        nc.gpsimd.memset(minus_half[:], -0.5)

        for r in range(0, 3):
            one_round(r)
        nc.vector.tensor_scalar_mul(
            out=sin_sb[:, :, 0:HALF], in0=sin_sb[:, :, 0:HALF], scalar1=-1.0
        )
        def rotate1(u):
            rotate(u, (0,))
        def rotate2(u):
            rotate(u, (1,))
        for r in range(3, 31):
            one_round(r)
        products(31)
        qk_to_tokens(26)
        copy_v(31)
        mean_squares(31)
        raise_to_power(31)
        other_tap(27, 0)
        rotated(25)
        qk_to_channels(28)
        last_tap(28)
        v_to_tokens(29)
        other_tap(27, 1)
        rotate1(26)
        normalise(30)
        other_tap(27, 2)
        gate(27)
        qk_to_channels(29)
        qk_to_tokens(27)
        last_tap(29)
        rotate2(26)
        other_tap(28, 0)
        finish_v(29)
        other_tap(28, 1)
        rotated(26)
        normalise(31)
        rotate1(27)
        other_tap(28, 2)
        qk_to_channels(30, "qk", 3)
        qk_to_channels(31, "qk", 3)
        rotate2(27)
        gate(28)
        last_tap(30)
        last_tap(31)
        other_tap(29, 0)
        v_products(30, SCALAR)
        qk_to_tokens(28)
        other_tap(29, 1)
        v_to_tokens(30)
        rotate1(28)
        other_tap(29, 2)
        gate(29)
        rotate2(28)
        other_tap(30, 0)
        other_tap(31, 0)
        v_products(31, SCALAR)
        qk_to_tokens(29)
        rotated(27)
        other_tap(30, 1)
        other_tap(31, 1)
        other_tap(30, 2)
        other_tap(31, 2)
        gate(30)
        gate(31)
        v_to_tokens(31)
        qk_to_tokens(30)
        rotate(29)
        rotated(28)
        finish_v(30)
        qk_to_tokens(31)
        rotate(30)
        rotated(29)
        finish_v(31)
        rotate(31)
        rotated(30)
        rotated(31)
